import numpy as np
import ml_dtypes


def mxq(x, axis, fmt="e4m3"):
    dtype, down = {"e4m3": (ml_dtypes.float8_e4m3fn, 7), "e5m2": (ml_dtypes.float8_e5m2, 14)}[fmt]
    v = np.moveaxis(np.asarray(x, np.float32).astype(ml_dtypes.bfloat16).astype(np.float64), axis, -1)
    blocks = v.reshape(v.shape[:-1] + (-1, 32))
    amax = np.abs(blocks).max(-1, keepdims=True)
    byte = np.maximum(np.where(amax > 0, np.frexp(amax)[1] - 1 + 127, 0) - down, 1)
    scale = np.exp2(byte - 127.0)
    codes = (blocks / scale).astype(np.float32).astype(dtype).astype(np.float64)
    return np.moveaxis((codes * scale).reshape(v.shape), -1, axis)


WIDE = False


def mx_kscale(k):
    if not WIDE:
        return np.ones(k)
    levels = np.array([10, -10, 5, -5, 0])
    if k % 512:
        return np.exp2(np.random.permutation(np.resize(levels, k // 32))).repeat(32)
    a = np.empty((k // 512, 16))
    for p in range(k // 512):
        a[p, :8] = np.random.permutation(np.resize(levels, 8))
        for g in range(8):
            far = levels[np.abs(levels - a[p, g]) >= 10]
            a[p, g + 8] = far[np.random.randint(len(far))]
    return np.exp2(a.ravel()).repeat(32)


BF16 = ml_dtypes.bfloat16


def bf(x):
    return np.asarray(x, np.float32).astype(BF16)


def f64(x):
    return np.asarray(x).astype(np.float64)


B, CIN, H, W, CR, COUT, SP, K = 4, 512, 32, 32, 512, 1024, 32, 7
PAD = K // 2
KK = K * K
HN = COUT // SP
HW = H * W
OFFS = [(dy, dx) for dy in range(K) for dx in range(K)]


def setup_inputs():
    s = mx_kscale(CIN)
    return {
        "logits": bf(np.random.standard_normal((B, HN, KK, HW)) * 1.5),
        "x": bf(np.random.standard_normal((B, CIN, H, W)) * s[None, :, None, None]),
        "w3c": bf(np.random.standard_normal((COUT, CIN)) * 2.0 / np.sqrt(CIN) / s[None, :]),
        "b3c": bf(np.random.standard_normal(COUT) * 0.5),
    }


def reference(logits, x, w3c, b3c):
    x3 = (mxq(f64(w3c), 1, "e4m3") @ mxq(f64(x).reshape(B, CIN, HW), 1, "e4m3")) + f64(b3c)[None, :, None]
    x3 = x3.reshape(B, COUT, H, W)
    lg = f64(logits)
    e = np.exp(lg - lg.max(axis=2, keepdims=True))
    wgt = (e / e.sum(axis=2, keepdims=True)).reshape(B, HN, KK, H, W)
    x3p = np.pad(x3, ((0, 0), (0, 0), (PAD, PAD), (PAD, PAD)), mode="reflect")
    acc = np.zeros((B, HN, SP, H, W))
    for k, (dy, dx) in enumerate(OFFS):
        patch = x3p[:, :, dy:dy + H, dx:dx + W].reshape(B, HN, SP, H, W)
        acc = acc + patch * wgt[:, :, k][:, :, None]
    return acc.reshape(B, COUT, H, W)

@@ -1,0 +1,358 @@
+from contextlib import ExitStack
+
+import concourse.mybir as mybir
+from concourse.masks import make_identity
+
+F32 = mybir.dt.float32
+BF16 = mybir.dt.bfloat16
+U32 = mybir.dt.uint32
+U8 = mybir.dt.uint8
+FP8X4 = mybir.dt.float8_e4m3fn_x4
+ALU = mybir.AluOpType
+ACTF = mybir.ActivationFunctionType
+AX = mybir.AxisListType
+
+P = 128
+NB = 4
+CIN = 512
+PACK = 4
+SIDE = 32
+COUT = 1024
+SP = 32
+NHEAD = COUT // SP
+KW = 7
+PAD = KW // 2
+KK = KW * KW
+ROWS = P // NHEAD
+NCHUNK = SIDE // ROWS
+HALF = 512
+HEADS = HALF // SP
+NACC = HALF // P
+WIDE = SIDE + 2 * PAD
+UNITS = 2 * ROWS * KW
+
+DX_VEC = 5
+DX_SCA = KW - DX_VEC
+DY_SUM = 5
+
+FLOPS = 2 * NB * COUT * CIN * SIDE * SIDE + 2 * NB * COUT * SIDE * SIDE * KK
+
+
+def reflect(u):
+    if u < 0:
+        return -u
+    if u > SIDE - 1:
+        return 2 * (SIDE - 1) - u
+    return u
+
+
+def tile_sam_pb_t_kernel(tc, logits, x, w3c, b3c, out):
+    nc = tc.nc
+    with ExitStack() as ctx:
+        ctx.enter_context(tc.manual_schedule())
+        const = ctx.enter_context(tc.tile_pool(name="const", bufs=1))
+        soft = ctx.enter_context(tc.tile_pool(name="soft", bufs=1))
+        wsp = ctx.enter_context(tc.tile_pool(name="wsp", bufs=2))
+        outp = ctx.enter_context(tc.tile_pool(name="outp", bufs=2))
+        psa = ctx.enter_context(tc.psum_pool(name="psa", bufs=2))
+        psb = ctx.enter_context(tc.psum_pool(name="psb", bufs=1))
+        psacc = ctx.enter_context(tc.psum_pool(name="psacc", bufs=1))
+        pswt = ctx.enter_context(tc.psum_pool(name="pswt", bufs=1))
+
+        xq = const.tile([P, SIDE * P], U32, align_bytes=64)
+        xs = const.tile([P, SIDE * P], U8, align_bytes=64)
+        wq = const.tile([P, COUT], U32, align_bytes=64)
+        wsc = const.tile([P, COUT], U8, align_bytes=64)
+        perm = const.tile([P, 3 * P], F32)
+        ident_bf = const.tile([P, P], BF16)
+        bias_sb = const.tile([P, COUT // P], F32)
+        wpad = const.tile([P, KK, WIDE, NB], F32)
+
+        logit_tiles = []
+        weight_tiles = []
+        cur = {}
+
+        def load_logits(ic):
+            lg = soft.tile([P, NB, KK, SIDE], BF16, name="lg")
+            for q in range(ROWS):
+                row = ROWS * ic + q
+                for b in range(NB):
+                    nc.sync.dma_start(
+                        out=lg[NHEAD * q : NHEAD * q + NHEAD, b],
+                        in_=logits[b, :, :, SIDE * row : SIDE * row + SIDE],
+                    )
+            logit_tiles.append(lg)
+
+        def fold_mirrored_columns():
+            w5 = wpad[:].rearrange("p (y d) j b -> p y d j b", d=KW)
+            for j in list(range(PAD)) + list(range(SIDE - PAD, SIDE)):
+                for dx in range(KW):
+                    c = j + dx - PAD
+                    if c != reflect(c):
+                        dxm = reflect(c) - j + PAD
+                        nc.vector.tensor_tensor(
+                            out=w5[:, :, dxm, PAD + j, :],
+                            in0=w5[:, :, dxm, PAD + j, :],
+                            in1=w5[:, :, dx, PAD + j, :],
+                            op=ALU.add,
+                        )
+
+        def transpose_weights(k, pool, name):
+            if k == 0:
+                weight_tiles.append(wsp.tile([P, KK, P], F32, name="ws"))
+            ws = weight_tiles[-1]
+            flat = wpad[:].rearrange("p l j b -> p l (j b)")
+            l0 = 4 * k
+            n = min(4, KK - l0)
+            wt = pool.tile([P, 4, P], F32, name=name)
+            for r in range(n):
+                first = NB * (2 * PAD - (l0 + r) % KW)
+                nc.tensor.transpose(wt[:, r, :], flat[:, l0 + r, first : first + P], perm[:, P : 2 * P])
+            nc.scalar.copy(out=ws[:, l0 : l0 + n, :], in_=wt[:, 0:n, :])
+
+        def prepare(ic, k):
+            if k < 8:
+                if k == 0:
+                    cur["max"] = soft.tile([P, NB, SIDE], F32, name="mx")
+                    cur["neg"] = soft.tile([P, NB, SIDE], F32, name="ng")
+                    cur["exp"] = soft.tile([P, NB, SIDE, KK], F32, name="ex")
+                    cur["sum"] = soft.tile([P, NB, SIDE], F32, name="sm")
+                b = k // 2
+                j0 = 16 * (k % 2)
+                nc.vector.tensor_reduce(
+                    out=cur["max"][:, b, j0 : j0 + 16],
+                    in_=logit_tiles[ic][:, b, :, j0 : j0 + 16].rearrange("p l j -> p j l"),
+                    axis=AX.X,
+                    op=ALU.max,
+                )
+                nc.vector.tensor_scalar_mul(
+                    out=cur["neg"][:, b, j0 : j0 + 16], in0=cur["max"][:, b, j0 : j0 + 16], scalar1=-1.0
+                )
+            elif k < 24:
+                for col in range(8 * (k - 8), 8 * (k - 8) + 8):
+                    b = col // SIDE
+                    j = col % SIDE
+                    nc.scalar.activation(
+                        out=cur["exp"][:, b, j, :],
+                        in_=logit_tiles[ic][:, b, :, j],
+                        func=ACTF.Exp,
+                        bias=cur["neg"][:, b, j : j + 1],
+                        scale=1.0,
+                        accum_out=cur["sum"][:, b, j : j + 1],
+                    )
+            elif k == 24:
+                cur["inv"] = soft.tile([P, NB, SIDE], F32, name="rs")
+                nc.vector.reciprocal(out=cur["inv"][:], in_=cur["sum"][:])
+                if ic + 1 < NCHUNK:
+                    load_logits(ic + 1)
+            elif k < 38:
+                if k % 2 == 1:
+                    dy = (k - 25) // 2
+                    eng = nc.vector if ic == 0 else nc.gpsimd
+                    eng.tensor_tensor(
+                        out=wpad[:, KW * dy : KW * dy + KW, PAD : PAD + SIDE, :],
+                        in0=cur["exp"][:, :, :, KW * dy : KW * dy + KW].rearrange("p b j l -> p l j b"),
+                        in1=cur["inv"][:].rearrange("p b j -> p j b").unsqueeze(1).to_broadcast([P, KW, SIDE, NB]),
+                        op=ALU.mult,
+                    )
+            elif k == 38:
+                fold_mirrored_columns()
+            elif k < 52:
+                if ic == 0:
+                    transpose_weights(k - 39, psacc, "acc%d" % (k % NACC))
+                else:
+                    transpose_weights(k - 39, pswt, "wt")
+
+        make_identity(nc, ident_bf[:])
+        make_identity(nc, perm[:, 0:P])
+        nc.gpsimd.memset(wpad[:], 0.0)
+        nc.vector.tensor_copy(out=perm[:, P : 2 * P], in_=perm[:, 0:P])
+        nc.vector.tensor_copy(out=perm[:, 2 * P : 3 * P], in_=perm[:, 0:P])
+
+        load_logits(0)
+
+        with tc.tile_pool(name="stage", bufs=1) as stage:
+            w_sb = stage.tile([P, COUT // P, CIN], BF16)
+            nc.scalar.dma_start(out=w_sb[:], in_=w3c.rearrange("(g p) c -> p g c", p=P))
+            b_rows = stage.tile([P, P], BF16)
+            nc.vector.memset(b_rows[:], 0.0)
+            nc.scalar.dma_start(out=b_rows[0 : COUT // P, :], in_=b3c.rearrange("(g o) -> g o", g=COUT // P))
+            x_sb = stage.tile([P, PACK, NB, SIDE * SIDE], BF16)
+            for b in range(NB):
+                nc.scalar.dma_start(out=x_sb[:, :, b, :], in_=x[b].rearrange("(p t) i j -> p t (i j)", t=PACK))
+
+            w_grp = stage.tile([P, COUT // P, P, PACK], BF16, align_bytes=64)
+            for g in range(COUT // P):
+                wtb = pswt.tile([P, PACK, P], BF16, name="wt")
+                for t in range(PACK):
+                    nc.tensor.transpose(wtb[:, t, :], w_sb[:, g, t : CIN : PACK], ident_bf[:])
+                nc.scalar.copy(out=w_grp[:, g], in_=wtb[:].rearrange("p t o -> p o t"))
+            btp = pswt.tile([P, P], BF16, name="wt")
+            nc.tensor.transpose(btp[:], b_rows[:], ident_bf[:])
+
+            for k in range(8):
+                prepare(0, k)
+                prepare(0, 8 + 2 * k)
+                prepare(0, 9 + 2 * k)
+
+            nc.vector.tensor_copy(out=bias_sb[:], in_=btp[:, 0 : COUT // P])
+            nc.vector.quantize_mx(
+                out=wq[:].bitcast(FP8X4),
+                scales=wsc[:],
+                in_=w_grp[:].rearrange("p g o t -> p (g o t)"),
+            )
+
+            for part in range(4):
+                xg = stage.tile([P, 256, NB, PACK], BF16, align_bytes=64, name="xg", bufs=2)
+                for b in range(NB):
+                    nc.vector.tensor_copy(
+                        out=xg[:, :, b, :],
+                        in_=x_sb[:, :, b, 256 * part : 256 * part + 256].rearrange("p t n -> p n t"),
+                    )
+                nc.vector.quantize_mx(
+                    out=xq[:, 1024 * part : 1024 * part + 1024].bitcast(FP8X4),
+                    scales=xs[:, 1024 * part : 1024 * part + 1024],
+                    in_=xg[:].rearrange("p n b t -> p (n b t)"),
+                )
+
+            for k in range(24, UNITS):
+                prepare(0, k)
+
+        qvp = ctx.enter_context(tc.tile_pool(name="qvp", bufs=4))
+        qap = ctx.enter_context(tc.tile_pool(name="qap", bufs=3))
+        csp = ctx.enter_context(tc.tile_pool(name="csp", bufs=2))
+        xcp = ctx.enter_context(tc.tile_pool(name="xcp", bufs=2))
+
+        units = []
+        for ic in range(NCHUNK):
+            for half in range(2):
+                for q in range(ROWS):
+                    for dy in range(KW):
+                        units.append((ic, half, q, dy))
+        nu = len(units)
+        x3_vector = []
+        prod_vector = []
+        prod_scalar = []
+        sums = []
+
+        def x3_pass(u, pool, name):
+            ic, half, q, dy = units[u]
+            a = reflect(ROWS * ic + q + dy - PAD)
+            xt = pool.tile([P, HALF], F32, name=name)
+            nc.tensor.matmul_mx(
+                out=xt[:],
+                lhsT=xq[:, P * a : P * a + P].bitcast(FP8X4),
+                lhsT_scale=xs[:, P * a : P * a + P],
+                rhs=wq[:, HALF * half : HALF * half + HALF].bitcast(FP8X4),
+                rhs_scale=wsc[:, HALF * half : HALF * half + HALF],
+                start=True,
+                stop=True,
+            )
+            return xt
+
+        def vector_part(u):
+            ic, half, q, dy = units[u]
+            h0 = NHEAD * q + HEADS * half
+            qv = qvp.tile([P, DX_VEC, HALF], F32, name="qv")
+            nc.vector.tensor_tensor(
+                out=qv[:].rearrange("p d (h c) -> p d h c", c=SP),
+                in0=x3_vector[u][:]
+                .rearrange("p (h c) -> p h c", c=SP)
+                .unsqueeze(1)
+                .to_broadcast([P, DX_VEC, HEADS, SP]),
+                in1=weight_tiles[ic][:, KW * dy : KW * dy + DX_VEC, h0 : h0 + HEADS]
+                .unsqueeze(3)
+                .to_broadcast([P, DX_VEC, HEADS, SP]),
+                op=ALU.mult,
+            )
+            prod_vector.append(qv)
+
+        def scalar_part(u):
+            ic, half, q, dy = units[u]
+            h0 = NHEAD * q + HEADS * half
+            xb = x3_pass(u, psb, "xb")
+            xc = xcp.tile([P, HALF], F32, name="xc")
+            nc.scalar.copy(out=xc[:], in_=xb[:])
+            if dy == 0:
+                qa = csp.tile([P, DX_SCA, HALF], F32, name="cs")
+                sums.append(qa)
+            else:
+                qa = qap.tile([P, DX_SCA, HALF], F32, name="qa")
+            for d in range(DX_SCA):
+                for h in range(HEADS):
+                    nc.scalar.activation(
+                        out=qa[:, d, SP * h : SP * h + SP],
+                        in_=xc[:, SP * h : SP * h + SP],
+                        func=ACTF.Copy,
+                        scale=weight_tiles[ic][:, KW * dy + DX_VEC + d, h0 + h : h0 + h + 1],
+                    )
+            if 0 < dy < DY_SUM:
+                nc.gpsimd.tensor_tensor(out=sums[-1][:], in0=sums[-1][:], in1=qa[:], op=ALU.add)
+            prod_scalar.append(qa)
+
+        def add_up(u, accs):
+            dy = units[u][3]
+            terms = []
+            for dx in range(DX_VEC):
+                terms.append((dx, prod_vector[u][:, dx, :]))
+            if dy >= DY_SUM:
+                for d in range(DX_SCA):
+                    terms.append((DX_VEC + d, prod_scalar[u][:, d, :]))
+            if dy == KW - 1:
+                for d in range(DX_SCA):
+                    terms.append((DX_VEC + d, sums[u // KW][:, d, :]))
+            for g in range(NACC):
+                for n, (dx, term) in enumerate(terms):
+                    shift = NB * (dx - PAD)
+                    nc.tensor.matmul(
+                        out=accs[g][:],
+                        lhsT=term[:, P * g : P * g + P],
+                        rhs=perm[:, P + shift : 2 * P + shift],
+                        start=(dy == 0 and n == 0),
+                        stop=(dy == KW - 1 and n == len(terms) - 1),
+                        is_transpose=True,
+                    )
+
+        x3_vector.append(x3_pass(0, psa, "xa"))
+        x3_vector.append(x3_pass(1, psa, "xa"))
+        for v in range(3):
+            scalar_part(v)
+        vector_part(0)
+        accs = []
+        osb = None
+        for u in range(nu):
+            ic, half, q, dy = units[u]
+            if u + 2 < nu:
+                x3_vector.append(x3_pass(u + 2, psa, "xa"))
+            if u + 3 < nu:
+                scalar_part(u + 3)
+            if u + 1 < nu:
+                vector_part(u + 1)
+            if dy == 0:
+                accs = []
+                for g in range(NACC):
+                    accs.append(psacc.tile([P, P], F32, name="acc%d" % g))
+            add_up(u, accs)
+            if dy == KW - 1:
+                if q == 0:
+                    osb = outp.tile([P, NACC, NB, ROWS, SIDE], F32, name="osb")
+                for g in range(NACC):
+                    gg = NACC * half + g
+                    nc.scalar.activation(
+                        out=osb[:, g, :, q, :],
+                        in_=accs[g][:].rearrange("o (j b) -> o b j", b=NB),
+                        func=ACTF.Identity,
+                        bias=bias_sb[:, gg : gg + 1],
+                        scale=1.0,
+                    )
+                if q == ROWS - 1:
+                    for g in range(NACC):
+                        gg = NACC * half + g
+                        nc.sync.dma_start(
+                            out=out[:, P * gg : P * gg + P, ROWS * ic : ROWS * ic + ROWS, :].rearrange(
+                                "b o q j -> o b (q j)"
+                            ),
+                            in_=osb[:, g].rearrange("o b q j -> o b (q j)"),
+                        )
+            if ic + 1 < NCHUNK:
+                prepare(ic + 1, u % UNITS)

@@ -19,21 +19,25 @@ PACK = 4
 SIDE = 32
 COUT = 1024
 SP = 32
-NHEAD = COUT // SP
 KW = 7
 PAD = KW // 2
 KK = KW * KW
-ROWS = P // NHEAD
-NCHUNK = SIDE // ROWS
-HALF = 512
-HEADS = HALF // SP
-NACC = HALF // P
 WIDE = SIDE + 2 * PAD
-UNITS = 2 * ROWS * KW
 
-DX_VEC = 5
-DX_SCA = KW - DX_VEC
-DY_SUM = 5
+BANK = 512
+CB = 256
+NBLK = COUT // CB
+HEADS = CB // SP
+NT = CB // P
+GROUP = BANK // CB
+ROWS = P // HEADS
+NCHUNK = SIDE // ROWS
+RING = 12
+STORE = 4
+
+DX_VEC = 4
+DX_SCA = 2
+DX_GPS = KW - 1
 
 FLOPS = 2 * NB * COUT * CIN * SIDE * SIDE + 2 * NB * COUT * SIDE * SIDE * KK
 
@@ -46,6 +50,10 @@ def reflect(u):
     return u
 
 
+def source_rows(i):
+    return sorted(set(reflect(i + dy - PAD) for dy in range(KW)))
+
+
 def tile_sam_pb_t_kernel(tc, logits, x, w3c, b3c, out):
     nc = tc.nc
     with ExitStack() as ctx:
@@ -53,11 +61,9 @@ def tile_sam_pb_t_kernel(tc, logits, x, w3c, b3c, out):
         const = ctx.enter_context(tc.tile_pool(name="const", bufs=1))
         soft = ctx.enter_context(tc.tile_pool(name="soft", bufs=1))
         wsp = ctx.enter_context(tc.tile_pool(name="wsp", bufs=2))
-        outp = ctx.enter_context(tc.tile_pool(name="outp", bufs=2))
         psa = ctx.enter_context(tc.psum_pool(name="psa", bufs=2))
-        psb = ctx.enter_context(tc.psum_pool(name="psb", bufs=1))
-        psacc = ctx.enter_context(tc.psum_pool(name="psacc", bufs=1))
-        pswt = ctx.enter_context(tc.psum_pool(name="pswt", bufs=1))
+        psacc = ctx.enter_context(tc.psum_pool(name="psacc", bufs=5))
+        psaux = ctx.enter_context(tc.psum_pool(name="psaux", bufs=1))
 
         xq = const.tile([P, SIDE * P], U32, align_bytes=64)
         xs = const.tile([P, SIDE * P], U8, align_bytes=64)
@@ -68,22 +74,71 @@ def tile_sam_pb_t_kernel(tc, logits, x, w3c, b3c, out):
         bias_sb = const.tile([P, COUT // P], F32)
         wpad = const.tile([P, KK, WIDE, NB], F32)
 
+        chunks = [(blk, ic) for blk in range(NBLK) for ic in range(NCHUNK)]
         logit_tiles = []
         weight_tiles = []
         cur = {}
 
-        def load_logits(ic):
+        def load_logits(n):
+            blk, ic = chunks[n]
             lg = soft.tile([P, NB, KK, SIDE], BF16, name="lg")
-            for q in range(ROWS):
-                row = ROWS * ic + q
+            for h in range(HEADS):
                 for b in range(NB):
                     nc.sync.dma_start(
-                        out=lg[NHEAD * q : NHEAD * q + NHEAD, b],
-                        in_=logits[b, :, :, SIDE * row : SIDE * row + SIDE],
+                        out=lg[ROWS * h : ROWS * h + ROWS, b],
+                        in_=logits[b, HEADS * blk + h, :, SIDE * ROWS * ic : SIDE * ROWS * (ic + 1)].rearrange(
+                            "l (q j) -> q l j", q=ROWS
+                        ),
                     )
             logit_tiles.append(lg)
 
-        def fold_mirrored_columns():
+        def column_maximum(n, k):
+            if k == 0:
+                cur["max"] = soft.tile([P, NB, SIDE], F32, name="mx")
+                cur["neg"] = soft.tile([P, NB, SIDE], F32, name="ng")
+                cur["exp"] = soft.tile([P, NB, SIDE, KK], F32, name="ex")
+                cur["sum"] = soft.tile([P, NB, SIDE], F32, name="sm")
+            b = k // 2
+            j0 = 16 * (k % 2)
+            nc.vector.tensor_reduce(
+                out=cur["max"][:, b, j0 : j0 + 16],
+                in_=logit_tiles[n][:, b, :, j0 : j0 + 16].rearrange("p l j -> p j l"),
+                axis=AX.X,
+                op=ALU.max,
+            )
+            nc.vector.tensor_scalar_mul(
+                out=cur["neg"][:, b, j0 : j0 + 16], in0=cur["max"][:, b, j0 : j0 + 16], scalar1=-1.0
+            )
+
+        def exponentials(n, k):
+            for col in range(8 * k, 8 * k + 8):
+                b = col // SIDE
+                j = col % SIDE
+                nc.scalar.activation(
+                    out=cur["exp"][:, b, j, :],
+                    in_=logit_tiles[n][:, b, :, j],
+                    func=ACTF.Exp,
+                    bias=cur["neg"][:, b, j : j + 1],
+                    scale=1.0,
+                    accum_out=cur["sum"][:, b, j : j + 1],
+                )
+
+        def reciprocal_sums(n, k):
+            cur["inv"] = soft.tile([P, NB, SIDE], F32, name="rs")
+            nc.vector.reciprocal(out=cur["inv"][:], in_=cur["sum"][:])
+            if n + 1 < len(chunks):
+                load_logits(n + 1)
+
+        def normalise(n, dy):
+            eng = nc.vector if n == 0 else nc.gpsimd
+            eng.tensor_tensor(
+                out=wpad[:, KW * dy : KW * dy + KW, PAD : PAD + SIDE, :],
+                in0=cur["exp"][:, :, :, KW * dy : KW * dy + KW].rearrange("p b j l -> p l j b"),
+                in1=cur["inv"][:].rearrange("p b j -> p j b").unsqueeze(1).to_broadcast([P, KW, SIDE, NB]),
+                op=ALU.mult,
+            )
+
+        def fold_mirrored_columns(n, k):
             w5 = wpad[:].rearrange("p (y d) j b -> p y d j b", d=KW)
             for j in list(range(PAD)) + list(range(SIDE - PAD, SIDE)):
                 for dx in range(KW):
@@ -97,71 +152,40 @@ def tile_sam_pb_t_kernel(tc, logits, x, w3c, b3c, out):
                             op=ALU.add,
                         )
 
-        def transpose_weights(k, pool, name):
+        def transpose_weights(n, k):
             if k == 0:
-                weight_tiles.append(wsp.tile([P, KK, P], F32, name="ws"))
-            ws = weight_tiles[-1]
+                weight_tiles.append(wsp.tile([P, KK, HEADS, ROWS], F32, name="ws"))
             flat = wpad[:].rearrange("p l j b -> p l (j b)")
             l0 = 4 * k
-            n = min(4, KK - l0)
-            wt = pool.tile([P, 4, P], F32, name=name)
-            for r in range(n):
+            m = min(4, KK - l0)
+            if n == 0:
+                wt = psacc.tile([P, 4, P], F32, name="acc")
+            else:
+                wt = psaux.tile([P, 4, P], F32, name="aux")
+            for r in range(m):
                 first = NB * (2 * PAD - (l0 + r) % KW)
                 nc.tensor.transpose(wt[:, r, :], flat[:, l0 + r, first : first + P], perm[:, P : 2 * P])
-            nc.scalar.copy(out=ws[:, l0 : l0 + n, :], in_=wt[:, 0:n, :])
+            nc.scalar.copy(
+                out=weight_tiles[n][:, l0 : l0 + m].rearrange("p l h q -> p l (h q)"), in_=wt[:, 0:m, :]
+            )
 
-        def prepare(ic, k):
-            if k < 8:
-                if k == 0:
-                    cur["max"] = soft.tile([P, NB, SIDE], F32, name="mx")
-                    cur["neg"] = soft.tile([P, NB, SIDE], F32, name="ng")
-                    cur["exp"] = soft.tile([P, NB, SIDE, KK], F32, name="ex")
-                    cur["sum"] = soft.tile([P, NB, SIDE], F32, name="sm")
-                b = k // 2
-                j0 = 16 * (k % 2)
-                nc.vector.tensor_reduce(
-                    out=cur["max"][:, b, j0 : j0 + 16],
-                    in_=logit_tiles[ic][:, b, :, j0 : j0 + 16].rearrange("p l j -> p j l"),
-                    axis=AX.X,
-                    op=ALU.max,
-                )
-                nc.vector.tensor_scalar_mul(
-                    out=cur["neg"][:, b, j0 : j0 + 16], in0=cur["max"][:, b, j0 : j0 + 16], scalar1=-1.0
-                )
-            elif k < 24:
-                for col in range(8 * (k - 8), 8 * (k - 8) + 8):
-                    b = col // SIDE
-                    j = col % SIDE
-                    nc.scalar.activation(
-                        out=cur["exp"][:, b, j, :],
-                        in_=logit_tiles[ic][:, b, :, j],
-                        func=ACTF.Exp,
-                        bias=cur["neg"][:, b, j : j + 1],
-                        scale=1.0,
-                        accum_out=cur["sum"][:, b, j : j + 1],
-                    )
-            elif k == 24:
-                cur["inv"] = soft.tile([P, NB, SIDE], F32, name="rs")
-                nc.vector.reciprocal(out=cur["inv"][:], in_=cur["sum"][:])
-                if ic + 1 < NCHUNK:
-                    load_logits(ic + 1)
-            elif k < 38:
-                if k % 2 == 1:
-                    dy = (k - 25) // 2
-                    eng = nc.vector if ic == 0 else nc.gpsimd
-                    eng.tensor_tensor(
-                        out=wpad[:, KW * dy : KW * dy + KW, PAD : PAD + SIDE, :],
-                        in0=cur["exp"][:, :, :, KW * dy : KW * dy + KW].rearrange("p b j l -> p l j b"),
-                        in1=cur["inv"][:].rearrange("p b j -> p j b").unsqueeze(1).to_broadcast([P, KW, SIDE, NB]),
-                        op=ALU.mult,
-                    )
-            elif k == 38:
-                fold_mirrored_columns()
-            elif k < 52:
-                if ic == 0:
-                    transpose_weights(k - 39, psacc, "acc%d" % (k % NACC))
-                else:
-                    transpose_weights(k - 39, pswt, "wt")
+        def fold_mirrored_rows(n, k):
+            ic = chunks[n][1]
+            w5 = weight_tiles[n][:].rearrange("p (y d) h q -> p y d h q", d=KW)
+            for q in range(ROWS):
+                i = ROWS * ic + q
+                for dy in range(KW):
+                    a = i + dy - PAD
+                    if a != reflect(a):
+                        dym = reflect(a) - i + PAD
+                        nc.vector.tensor_tensor(
+                            out=w5[:, dym, :, :, q], in0=w5[:, dym, :, :, q], in1=w5[:, dy, :, :, q], op=ALU.add
+                        )
+
+        softmax_steps = [(column_maximum, k) for k in range(8)] + [(exponentials, k) for k in range(16)]
+        weight_steps = [(reciprocal_sums, 0)] + [(normalise, k) for k in range(KW)] + [(fold_mirrored_columns, 0)]
+        weight_steps = weight_steps + [(transpose_weights, k) for k in range(13)] + [(fold_mirrored_rows, 0)]
+        steps = softmax_steps + weight_steps
 
         make_identity(nc, ident_bf[:])
         make_identity(nc, perm[:, 0:P])
@@ -183,17 +207,17 @@ def tile_sam_pb_t_kernel(tc, logits, x, w3c, b3c, out):
 
             w_grp = stage.tile([P, COUT // P, P, PACK], BF16, align_bytes=64)
             for g in range(COUT // P):
-                wtb = pswt.tile([P, PACK, P], BF16, name="wt")
+                wtb = psacc.tile([P, PACK, P], BF16, name="acc")
                 for t in range(PACK):
-                    nc.tensor.transpose(wtb[:, t, :], w_sb[:, g, t : CIN : PACK], ident_bf[:])
+                    nc.tensor.transpose(wtb[:, t, :], w_sb[:, g, t:CIN:PACK], ident_bf[:])
                 nc.scalar.copy(out=w_grp[:, g], in_=wtb[:].rearrange("p t o -> p o t"))
-            btp = pswt.tile([P, P], BF16, name="wt")
+            btp = psaux.tile([P, P], BF16, name="aux")
             nc.tensor.transpose(btp[:], b_rows[:], ident_bf[:])
 
             for k in range(8):
-                prepare(0, k)
-                prepare(0, 8 + 2 * k)
-                prepare(0, 9 + 2 * k)
+                column_maximum(0, k)
+                exponentials(0, 2 * k)
+                exponentials(0, 2 * k + 1)
 
             nc.vector.tensor_copy(out=bias_sb[:], in_=btp[:, 0 : COUT // P])
             nc.vector.quantize_mx(
@@ -215,144 +239,237 @@ def tile_sam_pb_t_kernel(tc, logits, x, w3c, b3c, out):
                     in_=xg[:].rearrange("p n b t -> p (n b t)"),
                 )
 
-            for k in range(24, UNITS):
-                prepare(0, k)
+            for step, k in weight_steps:
+                step(0, k)
 
-        qvp = ctx.enter_context(tc.tile_pool(name="qvp", bufs=4))
-        qap = ctx.enter_context(tc.tile_pool(name="qap", bufs=3))
-        csp = ctx.enter_context(tc.tile_pool(name="csp", bufs=2))
-        xcp = ctx.enter_context(tc.tile_pool(name="xcp", bufs=2))
+        ringp = ctx.enter_context(tc.tile_pool(name="ringp", bufs=1))
+        qvp = ctx.enter_context(tc.tile_pool(name="qvp", bufs=8))
+        qap = ctx.enter_context(tc.tile_pool(name="qap", bufs=10))
+        qgp = ctx.enter_context(tc.tile_pool(name="qgp", bufs=4))
+        gsp = ctx.enter_context(tc.tile_pool(name="gsp", bufs=5))
+        outp = ctx.enter_context(tc.tile_pool(name="outp", bufs=2))
 
-        units = []
-        for ic in range(NCHUNK):
-            for half in range(2):
-                for q in range(ROWS):
-                    for dy in range(KW):
-                        units.append((ic, half, q, dy))
-        nu = len(units)
-        x3_vector = []
-        prod_vector = []
-        prod_scalar = []
-        sums = []
+        bursts = []
+        chunk_bursts = []
+        for n, (blk, ic) in enumerate(chunks):
+            before = len(bursts)
+            for q in range(0, ROWS, GROUP):
+                rows = [ROWS * ic + q + r for r in range(GROUP)]
+                srcs = sorted(set(a for i in rows for a in source_rows(i)))
+                for s in range(0, len(srcs), GROUP):
+                    bursts.append((n, blk, rows, srcs[s : s + GROUP], s + GROUP >= len(srcs)))
+            chunk_bursts.append(len(bursts) - before)
+        nb = len(bursts)
 
-        def x3_pass(u, pool, name):
-            ic, half, q, dy = units[u]
-            a = reflect(ROWS * ic + q + dy - PAD)
-            xt = pool.tile([P, HALF], F32, name=name)
-            nc.tensor.matmul_mx(
-                out=xt[:],
-                lhsT=xq[:, P * a : P * a + P].bitcast(FP8X4),
-                lhsT_scale=xs[:, P * a : P * a + P],
-                rhs=wq[:, HALF * half : HALF * half + HALF].bitcast(FP8X4),
-                rhs_scale=wsc[:, HALF * half : HALF * half + HALF],
-                start=True,
-                stop=True,
-            )
-            return xt
+        ring = ringp.tile([P, RING, CB], F32)
+        in_ring = set()
+        x3_vector = {}
+        prod_vector = {}
+        prod_scalar = {}
+        prod_gpsimd = {}
+        sums = {}
+        accs = {}
+        stores = {}
+
+        def slot(a):
+            return (a + 1) % RING
+
+        def x3_passes(blk, srcs, tile):
+            for s, a in enumerate(srcs):
+                nc.tensor.matmul_mx(
+                    out=tile[:, s, :],
+                    lhsT=xq[:, P * a : P * a + P].bitcast(FP8X4),
+                    lhsT_scale=xs[:, P * a : P * a + P],
+                    rhs=wq[:, CB * blk : CB * blk + CB].bitcast(FP8X4),
+                    rhs_scale=wsc[:, CB * blk : CB * blk + CB],
+                    start=True,
+                    stop=True,
+                )
+
+        def x3_for_vector(u):
+            n, blk, rows, srcs, last = bursts[u]
+            xa = psa.tile([P, GROUP, CB], F32, name="xa")
+            x3_passes(blk, srcs, xa)
+            x3_vector[u] = xa
+
+        def x3_for_ring(u):
+            n, blk, rows, srcs, last = bursts[u]
+            new = [a for a in srcs if (blk, a) not in in_ring]
+            if len(new) > 0:
+                xb = psaux.tile([P, GROUP, CB], F32, name="aux")
+                x3_passes(blk, new, xb)
+                nc.scalar.copy(out=ring[:, slot(new[0]) : slot(new[0]) + len(new), :], in_=xb[:, 0 : len(new), :])
+                for a in new:
+                    in_ring.add((blk, a))
+
+        def readers(u):
+            n, blk, rows, srcs, last = bursts[u]
+            return [(s, i, a - i + PAD) for s, a in enumerate(srcs) for i in rows if a in source_rows(i)]
 
         def vector_part(u):
-            ic, half, q, dy = units[u]
-            h0 = NHEAD * q + HEADS * half
-            qv = qvp.tile([P, DX_VEC, HALF], F32, name="qv")
-            nc.vector.tensor_tensor(
-                out=qv[:].rearrange("p d (h c) -> p d h c", c=SP),
-                in0=x3_vector[u][:]
-                .rearrange("p (h c) -> p h c", c=SP)
-                .unsqueeze(1)
-                .to_broadcast([P, DX_VEC, HEADS, SP]),
-                in1=weight_tiles[ic][:, KW * dy : KW * dy + DX_VEC, h0 : h0 + HEADS]
-                .unsqueeze(3)
-                .to_broadcast([P, DX_VEC, HEADS, SP]),
-                op=ALU.mult,
-            )
-            prod_vector.append(qv)
+            n = bursts[u][0]
+            for s, i, dy in readers(u):
+                qv = qvp.tile([P, DX_VEC, CB], F32, name="qv")
+                nc.vector.tensor_tensor(
+                    out=qv[:].rearrange("p d (h c) -> p d h c", c=SP),
+                    in0=x3_vector[u][:, s, :]
+                    .rearrange("p (h c) -> p h c", c=SP)
+                    .unsqueeze(1)
+                    .to_broadcast([P, DX_VEC, HEADS, SP]),
+                    in1=weight_tiles[n][:, KW * dy : KW * dy + DX_VEC, :, i % ROWS]
+                    .unsqueeze(3)
+                    .to_broadcast([P, DX_VEC, HEADS, SP]),
+                    op=ALU.mult,
+                )
+                prod_vector[u, s, i] = qv
 
         def scalar_part(u):
-            ic, half, q, dy = units[u]
-            h0 = NHEAD * q + HEADS * half
-            xb = x3_pass(u, psb, "xb")
-            xc = xcp.tile([P, HALF], F32, name="xc")
-            nc.scalar.copy(out=xc[:], in_=xb[:])
-            if dy == 0:
-                qa = csp.tile([P, DX_SCA, HALF], F32, name="cs")
-                sums.append(qa)
-            else:
-                qa = qap.tile([P, DX_SCA, HALF], F32, name="qa")
-            for d in range(DX_SCA):
-                for h in range(HEADS):
-                    nc.scalar.activation(
-                        out=qa[:, d, SP * h : SP * h + SP],
-                        in_=xc[:, SP * h : SP * h + SP],
-                        func=ACTF.Copy,
-                        scale=weight_tiles[ic][:, KW * dy + DX_VEC + d, h0 + h : h0 + h + 1],
-                    )
-            if 0 < dy < DY_SUM:
-                nc.gpsimd.tensor_tensor(out=sums[-1][:], in0=sums[-1][:], in1=qa[:], op=ALU.add)
-            prod_scalar.append(qa)
-
-        def add_up(u, accs):
-            dy = units[u][3]
-            terms = []
-            for dx in range(DX_VEC):
-                terms.append((dx, prod_vector[u][:, dx, :]))
-            if dy >= DY_SUM:
+            n, blk, rows, srcs, last = bursts[u]
+            for s, i, dy in readers(u):
+                qa = qap.tile([P, DX_SCA, CB], F32, name="qa")
+                q = i % ROWS
                 for d in range(DX_SCA):
-                    terms.append((DX_VEC + d, prod_scalar[u][:, d, :]))
-            if dy == KW - 1:
-                for d in range(DX_SCA):
-                    terms.append((DX_VEC + d, sums[u // KW][:, d, :]))
-            for g in range(NACC):
-                for n, (dx, term) in enumerate(terms):
-                    shift = NB * (dx - PAD)
-                    nc.tensor.matmul(
-                        out=accs[g][:],
-                        lhsT=term[:, P * g : P * g + P],
-                        rhs=perm[:, P + shift : 2 * P + shift],
-                        start=(dy == 0 and n == 0),
-                        stop=(dy == KW - 1 and n == len(terms) - 1),
-                        is_transpose=True,
-                    )
+                    for h in range(HEADS):
+                        nc.scalar.activation(
+                            out=qa[:, d, SP * h : SP * h + SP],
+                            in_=ring[:, slot(srcs[s]), SP * h : SP * h + SP],
+                            func=ACTF.Copy,
+                            scale=weight_tiles[n][:, KW * dy + DX_VEC + d, h, q : q + 1],
+                        )
+                prod_scalar[u, s, i] = qa
 
-        x3_vector.append(x3_pass(0, psa, "xa"))
-        x3_vector.append(x3_pass(1, psa, "xa"))
-        for v in range(3):
-            scalar_part(v)
-        vector_part(0)
-        accs = []
-        osb = None
-        for u in range(nu):
-            ic, half, q, dy = units[u]
-            if u + 2 < nu:
-                x3_vector.append(x3_pass(u + 2, psa, "xa"))
-            if u + 3 < nu:
-                scalar_part(u + 3)
-            if u + 1 < nu:
-                vector_part(u + 1)
-            if dy == 0:
-                accs = []
-                for g in range(NACC):
-                    accs.append(psacc.tile([P, P], F32, name="acc%d" % g))
-            add_up(u, accs)
-            if dy == KW - 1:
-                if q == 0:
-                    osb = outp.tile([P, NACC, NB, ROWS, SIDE], F32, name="osb")
-                for g in range(NACC):
-                    gg = NACC * half + g
+        def gpsimd_part(u):
+            n, blk, rows, srcs, last = bursts[u]
+            w5 = weight_tiles[n][:].rearrange("p (y d) h q -> p y d h q", d=KW)
+            additions = []
+
+            def multiply(i, places, tile):
+                s0 = places[0]
+                m = len(places)
+                dy = srcs[s0] - i + PAD
+                nc.gpsimd.tensor_tensor(
+                    out=tile[:, s0 : s0 + m, :].rearrange("p s (h c) -> p s h c", c=SP),
+                    in0=ring[:, slot(srcs[s0]) : slot(srcs[s0]) + m, :].rearrange("p s (h c) -> p s h c", c=SP),
+                    in1=w5[:, dy : dy + m, DX_GPS, :, i % ROWS].unsqueeze(3).to_broadcast([P, m, HEADS, SP]),
+                    op=ALU.mult,
+                )
+
+            for i in rows:
+                places = [s for s, row, dy in readers(u) if row == i]
+                if (blk, i) not in sums:
+                    total = gsp.tile([P, GROUP, CB], F32, name="gs")
+                    sums[blk, i] = (total, set())
+                total, filled = sums[blk, i]
+                handed = []
+                if last:
+                    handed = [(total, s) for s in sorted(filled)]
+                    if len(places) > 0:
+                        qg = qgp.tile([P, GROUP, CB], F32, name="qg")
+                        multiply(i, places, qg)
+                        handed = handed + [(qg, s) for s in places]
+                else:
+                    fresh = [s for s in places if s not in filled]
+                    old = [s for s in places if s in filled]
+                    if len(old) > 0:
+                        qg = qgp.tile([P, GROUP, CB], F32, name="qg")
+                        multiply(i, old, qg)
+                        additions.append((total, qg, old))
+                    if len(fresh) > 0:
+                        multiply(i, fresh, total)
+                        for s in fresh:
+                            filled.add(s)
+                prod_gpsimd[u, i] = handed
+            for total, qg, places in additions:
+                s0 = places[0]
+                s1 = s0 + len(places)
+                nc.gpsimd.tensor_tensor(
+                    out=total[:, s0:s1, :], in0=total[:, s0:s1, :], in1=qg[:, s0:s1, :], op=ALU.add
+                )
+
+        def add_up(u):
+            n, blk, rows, srcs, last = bursts[u]
+            for i in rows:
+                places = [s for s, row, dy in readers(u) if row == i]
+                terms = []
+                for s in places:
+                    for d in range(DX_SCA):
+                        terms.append((DX_VEC + d, prod_scalar[u, s, i][:, d, :]))
+                for tile, s in prod_gpsimd[u, i]:
+                    terms.append((DX_GPS, tile[:, s, :]))
+                for s in places:
+                    for dx in range(DX_VEC):
+                        terms.append((dx, prod_vector[u, s, i][:, dx, :]))
+                for t in range(NT):
+                    opens = (blk, i, t) not in accs
+                    if opens:
+                        acc = psacc.tile([P, BANK], F32, name="acc")
+                        accs[blk, i, t] = acc
+                    for m, (dx, term) in enumerate(terms):
+                        shift = NB * (dx - PAD)
+                        nc.tensor.matmul(
+                            out=accs[blk, i, t][:, 0:P],
+                            lhsT=term[:, P * t : P * t + P],
+                            rhs=perm[:, P + shift : 2 * P + shift],
+                            start=(opens and m == 0),
+                            stop=(last and m == len(terms) - 1),
+                            is_transpose=True,
+                        )
+
+        def finish(u):
+            n, blk, rows, srcs, last = bursts[u]
+            if not last:
+                return
+            for i in rows:
+                if i % STORE == 0:
+                    osb = outp.tile([P, NT, NB, STORE, SIDE], F32, name="osb")
+                    stores[0] = osb
+                for t in range(NT):
+                    g = NT * blk + t
                     nc.scalar.activation(
-                        out=osb[:, g, :, q, :],
-                        in_=accs[g][:].rearrange("o (j b) -> o b j", b=NB),
+                        out=stores[0][:, t, :, i % STORE, :],
+                        in_=accs[blk, i, t][:, 0:P].rearrange("o (j b) -> o b j", b=NB),
                         func=ACTF.Identity,
-                        bias=bias_sb[:, gg : gg + 1],
+                        bias=bias_sb[:, g : g + 1],
                         scale=1.0,
                     )
-                if q == ROWS - 1:
-                    for g in range(NACC):
-                        gg = NACC * half + g
+                if i % STORE == STORE - 1:
+                    for t in range(NT):
+                        g = NT * blk + t
                         nc.sync.dma_start(
-                            out=out[:, P * gg : P * gg + P, ROWS * ic : ROWS * ic + ROWS, :].rearrange(
-                                "b o q j -> o b (q j)"
-                            ),
-                            in_=osb[:, g].rearrange("o b q j -> o b (q j)"),
+                            out=out[:, P * g : P * g + P, i - STORE + 1 : i + 1, :].rearrange("b o q j -> o b (q j)"),
+                            in_=stores[0][:, t].rearrange("o b q j -> o b (q j)"),
                         )
-            if ic + 1 < NCHUNK:
-                prepare(ic + 1, u % UNITS)
+
+        x3_for_vector(0)
+        x3_for_vector(1)
+        for v in range(3):
+            x3_for_ring(v)
+        for v in range(2):
+            scalar_part(v)
+            gpsimd_part(v)
+        vector_part(0)
+        done = 0
+        first = 0
+        for u in range(nb):
+            n = bursts[u][0]
+            if u > 0:
+                finish(u - 1)
+            if u + 2 < nb:
+                x3_for_vector(u + 2)
+            if u + 3 < nb:
+                x3_for_ring(u + 3)
+            if u + 2 < nb:
+                scalar_part(u + 2)
+                gpsimd_part(u + 2)
+            if u + 1 < nb:
+                vector_part(u + 1)
+            add_up(u)
+            if u > 0 and n != bursts[u - 1][0]:
+                done = 0
+                first = u
+            if n + 1 < len(chunks):
+                share = min(len(steps), len(steps) * (u - first + 1) // (chunk_bursts[n] - 3))
+                for step, k in steps[done:share]:
+                    step(n + 1, k)
+                done = share
+        finish(nb - 1)

@@ -23,6 +23,7 @@ KW = 7
 PAD = KW // 2
 KK = KW * KW
 WIDE = SIDE + 2 * PAD
+HALF = SIDE // 2
 
 BANK = 512
 CB = 256
@@ -35,9 +36,11 @@ NCHUNK = SIDE // ROWS
 RING = 12
 STORE = 4
 
-DX_VEC = 4
-DX_SCA = 2
-DX_GPS = KW - 1
+DX_VEC = 5
+DX_SCA = KW - DX_VEC
+SUM_VEC = 3
+
+REPEAT = 2
 
 FLOPS = 2 * NB * COUT * CIN * SIDE * SIDE + 2 * NB * COUT * SIDE * SIDE * KK
 
@@ -62,8 +65,9 @@ def tile_sam_pb_t_kernel(tc, logits, x, w3c, b3c, out):
         soft = ctx.enter_context(tc.tile_pool(name="soft", bufs=1))
         wsp = ctx.enter_context(tc.tile_pool(name="wsp", bufs=2))
         psa = ctx.enter_context(tc.psum_pool(name="psa", bufs=2))
-        psacc = ctx.enter_context(tc.psum_pool(name="psacc", bufs=5))
-        psaux = ctx.enter_context(tc.psum_pool(name="psaux", bufs=1))
+        psacc = ctx.enter_context(tc.psum_pool(name="psacc", bufs=4))
+        psring = ctx.enter_context(tc.psum_pool(name="psring", bufs=1))
+        pswt = ctx.enter_context(tc.psum_pool(name="pswt", bufs=1))
 
         xq = const.tile([P, SIDE * P], U32, align_bytes=64)
         xs = const.tile([P, SIDE * P], U8, align_bytes=64)
@@ -77,6 +81,7 @@ def tile_sam_pb_t_kernel(tc, logits, x, w3c, b3c, out):
         chunks = [(blk, ic) for blk in range(NBLK) for ic in range(NCHUNK)]
         logit_tiles = []
         weight_tiles = []
+        transposed = []
         cur = {}
 
         def load_logits(n):
@@ -92,30 +97,31 @@ def tile_sam_pb_t_kernel(tc, logits, x, w3c, b3c, out):
                     )
             logit_tiles.append(lg)
 
-        def column_maximum(n, k):
-            if k == 0:
+        def column_maximum(n, half, b):
+            if half == 0 and b == 0:
                 cur["max"] = soft.tile([P, NB, SIDE], F32, name="mx")
                 cur["neg"] = soft.tile([P, NB, SIDE], F32, name="ng")
-                cur["exp"] = soft.tile([P, NB, SIDE, KK], F32, name="ex")
                 cur["sum"] = soft.tile([P, NB, SIDE], F32, name="sm")
-            b = k // 2
-            j0 = 16 * (k % 2)
+                cur["inv"] = soft.tile([P, NB, SIDE], F32, name="rs")
+            j0 = HALF * half
             nc.vector.tensor_reduce(
-                out=cur["max"][:, b, j0 : j0 + 16],
-                in_=logit_tiles[n][:, b, :, j0 : j0 + 16].rearrange("p l j -> p j l"),
+                out=cur["max"][:, b, j0 : j0 + HALF],
+                in_=logit_tiles[n][:, b, :, j0 : j0 + HALF].rearrange("p l j -> p j l"),
                 axis=AX.X,
                 op=ALU.max,
             )
             nc.vector.tensor_scalar_mul(
-                out=cur["neg"][:, b, j0 : j0 + 16], in0=cur["max"][:, b, j0 : j0 + 16], scalar1=-1.0
+                out=cur["neg"][:, b, j0 : j0 + HALF], in0=cur["max"][:, b, j0 : j0 + HALF], scalar1=-1.0
             )
 
-        def exponentials(n, k):
-            for col in range(8 * k, 8 * k + 8):
-                b = col // SIDE
-                j = col % SIDE
+        def exponentials(n, half, k, pool=soft):
+            if k == 0:
+                cur["exp", half] = pool.tile([P, NB, HALF, KK], F32, name="ex")
+            b = k // 2
+            for m in range(8 * (k % 2), 8 * (k % 2) + 8):
+                j = HALF * half + m
                 nc.scalar.activation(
-                    out=cur["exp"][:, b, j, :],
+                    out=cur["exp", half][:, b, m, :],
                     in_=logit_tiles[n][:, b, :, j],
                     func=ACTF.Exp,
                     bias=cur["neg"][:, b, j : j + 1],
@@ -123,22 +129,25 @@ def tile_sam_pb_t_kernel(tc, logits, x, w3c, b3c, out):
                     accum_out=cur["sum"][:, b, j : j + 1],
                 )
 
-        def reciprocal_sums(n, k):
-            cur["inv"] = soft.tile([P, NB, SIDE], F32, name="rs")
-            nc.vector.reciprocal(out=cur["inv"][:], in_=cur["sum"][:])
-            if n + 1 < len(chunks):
+        def reciprocal_sums(n, half, k):
+            j0 = HALF * half
+            nc.vector.reciprocal(out=cur["inv"][:, :, j0 : j0 + HALF], in_=cur["sum"][:, :, j0 : j0 + HALF])
+            if half == 1 and n + 1 < len(chunks):
                 load_logits(n + 1)
 
-        def normalise(n, dy):
-            eng = nc.vector if n == 0 else nc.gpsimd
-            eng.tensor_tensor(
-                out=wpad[:, KW * dy : KW * dy + KW, PAD : PAD + SIDE, :],
-                in0=cur["exp"][:, :, :, KW * dy : KW * dy + KW].rearrange("p b j l -> p l j b"),
-                in1=cur["inv"][:].rearrange("p b j -> p j b").unsqueeze(1).to_broadcast([P, KW, SIDE, NB]),
+        def normalise(n, half, dy):
+            j0 = HALF * half
+            nc.vector.tensor_tensor(
+                out=wpad[:, KW * dy : KW * dy + KW, PAD + j0 : PAD + j0 + HALF, :],
+                in0=cur["exp", half][:, :, :, KW * dy : KW * dy + KW].rearrange("p b j l -> p l j b"),
+                in1=cur["inv"][:, :, j0 : j0 + HALF]
+                .rearrange("p b j -> p j b")
+                .unsqueeze(1)
+                .to_broadcast([P, KW, HALF, NB]),
                 op=ALU.mult,
             )
 
-        def fold_mirrored_columns(n, k):
+        def fold_mirrored_columns(n, half, k):
             w5 = wpad[:].rearrange("p (y d) j b -> p y d j b", d=KW)
             for j in list(range(PAD)) + list(range(SIDE - PAD, SIDE)):
                 for dx in range(KW):
@@ -152,7 +161,7 @@ def tile_sam_pb_t_kernel(tc, logits, x, w3c, b3c, out):
                             op=ALU.add,
                         )
 
-        def transpose_weights(n, k):
+        def transpose_weights(n, half, k):
             if k == 0:
                 weight_tiles.append(wsp.tile([P, KK, HEADS, ROWS], F32, name="ws"))
             flat = wpad[:].rearrange("p l j b -> p l (j b)")
@@ -161,15 +170,20 @@ def tile_sam_pb_t_kernel(tc, logits, x, w3c, b3c, out):
             if n == 0:
                 wt = psacc.tile([P, 4, P], F32, name="acc")
             else:
-                wt = psaux.tile([P, 4, P], F32, name="aux")
+                wt = pswt.tile([P, 4, P], F32, name="wt")
             for r in range(m):
                 first = NB * (2 * PAD - (l0 + r) % KW)
                 nc.tensor.transpose(wt[:, r, :], flat[:, l0 + r, first : first + P], perm[:, P : 2 * P])
-            nc.scalar.copy(
-                out=weight_tiles[n][:, l0 : l0 + m].rearrange("p l h q -> p l (h q)"), in_=wt[:, 0:m, :]
-            )
+            transposed.append((n, l0, m, wt))
 
-        def fold_mirrored_rows(n, k):
+        def copy_weights():
+            for n, l0, m, wt in transposed:
+                nc.scalar.copy(
+                    out=weight_tiles[n][:, l0 : l0 + m].rearrange("p l h q -> p l (h q)"), in_=wt[:, 0:m, :]
+                )
+            transposed.clear()
+
+        def fold_mirrored_rows(n, half, k):
             ic = chunks[n][1]
             w5 = weight_tiles[n][:].rearrange("p (y d) h q -> p y d h q", d=KW)
             for q in range(ROWS):
@@ -182,28 +196,34 @@ def tile_sam_pb_t_kernel(tc, logits, x, w3c, b3c, out):
                             out=w5[:, dym, :, :, q], in0=w5[:, dym, :, :, q], in1=w5[:, dy, :, :, q], op=ALU.add
                         )
 
-        softmax_steps = [(column_maximum, k) for k in range(8)] + [(exponentials, k) for k in range(16)]
-        weight_steps = [(reciprocal_sums, 0)] + [(normalise, k) for k in range(KW)] + [(fold_mirrored_columns, 0)]
-        weight_steps = weight_steps + [(transpose_weights, k) for k in range(13)] + [(fold_mirrored_rows, 0)]
-        steps = softmax_steps + weight_steps
+        softmax_steps = [(column_maximum, half, b) for half in range(2) for b in range(NB)]
+        for half in range(2):
+            softmax_steps = softmax_steps + [(exponentials, half, k) for k in range(2 * NB)]
+            softmax_steps = softmax_steps + [(reciprocal_sums, half, 0)] + [(normalise, half, dy) for dy in range(KW)]
+        weight_steps = [(fold_mirrored_columns, 0, 0)] + [(transpose_weights, 0, k) for k in range(13)]
+        weight_steps = weight_steps + [(fold_mirrored_rows, 0, 0)]
 
         make_identity(nc, ident_bf[:])
         make_identity(nc, perm[:, 0:P])
         nc.gpsimd.memset(wpad[:], 0.0)
-        nc.vector.tensor_copy(out=perm[:, P : 2 * P], in_=perm[:, 0:P])
-        nc.vector.tensor_copy(out=perm[:, 2 * P : 3 * P], in_=perm[:, 0:P])
-
-        load_logits(0)
 
         with tc.tile_pool(name="stage", bufs=1) as stage:
             w_sb = stage.tile([P, COUT // P, CIN], BF16)
-            nc.scalar.dma_start(out=w_sb[:], in_=w3c.rearrange("(g p) c -> p g c", p=P))
+            nc.sync.dma_start(out=w_sb[:], in_=w3c.rearrange("(g p) c -> p g c", p=P))
+            XP = 256
+            x_sb = stage.tile([P, 4, NB, PACK, XP], BF16)
+            for part in range(4):
+                for b in range(NB):
+                    nc.scalar.dma_start(
+                        out=x_sb[:, part, b],
+                        in_=x[b].rearrange("(p t) i j -> p t (i j)", t=PACK)[:, :, XP * part : XP * part + XP],
+                    )
+            load_logits(0)
             b_rows = stage.tile([P, P], BF16)
             nc.vector.memset(b_rows[:], 0.0)
             nc.scalar.dma_start(out=b_rows[0 : COUT // P, :], in_=b3c.rearrange("(g o) -> g o", g=COUT // P))
-            x_sb = stage.tile([P, PACK, NB, SIDE * SIDE], BF16)
-            for b in range(NB):
-                nc.scalar.dma_start(out=x_sb[:, :, b, :], in_=x[b].rearrange("(p t) i j -> p t (i j)", t=PACK))
+            nc.vector.tensor_copy(out=perm[:, P : 2 * P], in_=perm[:, 0:P])
+            nc.vector.tensor_copy(out=perm[:, 2 * P : 3 * P], in_=perm[:, 0:P])
 
             w_grp = stage.tile([P, COUT // P, P, PACK], BF16, align_bytes=64)
             for g in range(COUT // P):
@@ -211,42 +231,57 @@ def tile_sam_pb_t_kernel(tc, logits, x, w3c, b3c, out):
                 for t in range(PACK):
                     nc.tensor.transpose(wtb[:, t, :], w_sb[:, g, t:CIN:PACK], ident_bf[:])
                 nc.scalar.copy(out=w_grp[:, g], in_=wtb[:].rearrange("p t o -> p o t"))
-            btp = psaux.tile([P, P], BF16, name="aux")
+            btp = pswt.tile([P, P], BF16, name="wt")
             nc.tensor.transpose(btp[:], b_rows[:], ident_bf[:])
 
-            for k in range(8):
-                column_maximum(0, k)
-                exponentials(0, 2 * k)
-                exponentials(0, 2 * k + 1)
+            x_parts = []
 
-            nc.vector.tensor_copy(out=bias_sb[:], in_=btp[:, 0 : COUT // P])
+            def interleave(part):
+                xg = stage.tile([P, XP, NB, PACK], BF16, align_bytes=64, name="xg", bufs=2)
+                for b in range(NB):
+                    nc.vector.tensor_copy(out=xg[:, :, b, :], in_=x_sb[:, part, b].rearrange("p t n -> p n t"))
+                x_parts.append(xg)
+
+            def quantise(part):
+                n0 = XP * NB * part
+                nc.vector.quantize_mx(
+                    out=xq[:, n0 : n0 + XP * NB].bitcast(FP8X4),
+                    scales=xs[:, n0 : n0 + XP * NB],
+                    in_=x_parts[part][:].rearrange("p n b t -> p (n b t)"),
+                )
+
+            interleave(0)
+            for part in range(4):
+                if part + 1 < 4:
+                    interleave(part + 1)
+                quantise(part)
             nc.vector.quantize_mx(
                 out=wq[:].bitcast(FP8X4),
                 scales=wsc[:],
                 in_=w_grp[:].rearrange("p g o t -> p (g o t)"),
             )
+            nc.vector.tensor_copy(out=bias_sb[:], in_=btp[:, 0 : COUT // P])
 
-            for part in range(4):
-                xg = stage.tile([P, 256, NB, PACK], BF16, align_bytes=64, name="xg", bufs=2)
+            for half in range(2):
                 for b in range(NB):
-                    nc.vector.tensor_copy(
-                        out=xg[:, :, b, :],
-                        in_=x_sb[:, :, b, 256 * part : 256 * part + 256].rearrange("p t n -> p n t"),
-                    )
-                nc.vector.quantize_mx(
-                    out=xq[:, 1024 * part : 1024 * part + 1024].bitcast(FP8X4),
-                    scales=xs[:, 1024 * part : 1024 * part + 1024],
-                    in_=xg[:].rearrange("p n b t -> p (n b t)"),
-                )
-
-            for step, k in weight_steps:
-                step(0, k)
+                    column_maximum(0, half, b)
+            for half in range(2):
+                for k in range(2 * NB):
+                    exponentials(0, half, k, soft if half == 0 else stage)
+                reciprocal_sums(0, half, 0)
+                for dy in range(KW):
+                    normalise(0, half, dy)
+            fold_mirrored_columns(0, 0, 0)
+            for k in range(13):
+                transpose_weights(0, 0, k)
+                copy_weights()
+            fold_mirrored_rows(0, 0, 0)
 
         ringp = ctx.enter_context(tc.tile_pool(name="ringp", bufs=1))
-        qvp = ctx.enter_context(tc.tile_pool(name="qvp", bufs=8))
-        qap = ctx.enter_context(tc.tile_pool(name="qap", bufs=10))
-        qgp = ctx.enter_context(tc.tile_pool(name="qgp", bufs=4))
-        gsp = ctx.enter_context(tc.tile_pool(name="gsp", bufs=5))
+        qvp = ctx.enter_context(tc.tile_pool(name="qvp", bufs=5))
+        qsp = ctx.enter_context(tc.tile_pool(name="qsp", bufs=3))
+        ssp = ctx.enter_context(tc.tile_pool(name="ssp", bufs=4))
+        svp = ctx.enter_context(tc.tile_pool(name="svp", bufs=3))
         outp = ctx.enter_context(tc.tile_pool(name="outp", bufs=2))
 
         bursts = []
@@ -257,22 +292,31 @@ def tile_sam_pb_t_kernel(tc, logits, x, w3c, b3c, out):
                 rows = [ROWS * ic + q + r for r in range(GROUP)]
                 srcs = sorted(set(a for i in rows for a in source_rows(i)))
                 for s in range(0, len(srcs), GROUP):
-                    bursts.append((n, blk, rows, srcs[s : s + GROUP], s + GROUP >= len(srcs)))
+                    bursts.append((n, blk, rows, srcs[s : s + GROUP], s // GROUP, s + GROUP >= len(srcs)))
             chunk_bursts.append(len(bursts) - before)
         nb = len(bursts)
 
         ring = ringp.tile([P, RING, CB], F32)
         in_ring = set()
+        ring_copies = []
         x3_vector = {}
         prod_vector = {}
         prod_scalar = {}
-        prod_gpsimd = {}
-        sums = {}
+        sum_vector = {}
+        sum_scalar = {}
+        direct_vector = set()
+        direct_scalar = set()
         accs = {}
-        stores = {}
+        store = {}
 
         def slot(a):
             return (a + 1) % RING
+
+        def places_of(u, i):
+            places = [s for s, a in enumerate(bursts[u][3]) if a in source_rows(i)]
+            if len(places) == 0:
+                return 0, 0
+            return places[0], places[-1] + 1
 
         def x3_passes(blk, srcs, tile):
             for s, a in enumerate(srcs):
@@ -287,118 +331,112 @@ def tile_sam_pb_t_kernel(tc, logits, x, w3c, b3c, out):
                 )
 
         def x3_for_vector(u):
-            n, blk, rows, srcs, last = bursts[u]
+            n, blk, rows, srcs, number, last = bursts[u]
             xa = psa.tile([P, GROUP, CB], F32, name="xa")
-            x3_passes(blk, srcs, xa)
+            for k in range(REPEAT):
+                x3_passes(blk, srcs, xa)
             x3_vector[u] = xa
 
         def x3_for_ring(u):
-            n, blk, rows, srcs, last = bursts[u]
+            n, blk, rows, srcs, number, last = bursts[u]
             new = [a for a in srcs if (blk, a) not in in_ring]
             if len(new) > 0:
-                xb = psaux.tile([P, GROUP, CB], F32, name="aux")
+                xb = psring.tile([P, GROUP, CB], F32, name="xb")
                 x3_passes(blk, new, xb)
-                nc.scalar.copy(out=ring[:, slot(new[0]) : slot(new[0]) + len(new), :], in_=xb[:, 0 : len(new), :])
+                ring_copies.append((new, xb))
                 for a in new:
                     in_ring.add((blk, a))
 
-        def readers(u):
-            n, blk, rows, srcs, last = bursts[u]
-            return [(s, i, a - i + PAD) for s, a in enumerate(srcs) for i in rows if a in source_rows(i)]
+        def copy_ring():
+            for new, xb in ring_copies:
+                s0 = slot(new[0])
+                nc.scalar.copy(out=ring[:, s0 : s0 + len(new), :], in_=xb[:, 0 : len(new), :])
+            ring_copies.clear()
 
         def vector_part(u):
-            n = bursts[u][0]
-            for s, i, dy in readers(u):
-                qv = qvp.tile([P, DX_VEC, CB], F32, name="qv")
-                nc.vector.tensor_tensor(
-                    out=qv[:].rearrange("p d (h c) -> p d h c", c=SP),
-                    in0=x3_vector[u][:, s, :]
-                    .rearrange("p (h c) -> p h c", c=SP)
-                    .unsqueeze(1)
-                    .to_broadcast([P, DX_VEC, HEADS, SP]),
-                    in1=weight_tiles[n][:, KW * dy : KW * dy + DX_VEC, :, i % ROWS]
-                    .unsqueeze(3)
-                    .to_broadcast([P, DX_VEC, HEADS, SP]),
-                    op=ALU.mult,
-                )
-                prod_vector[u, s, i] = qv
+            n, blk, rows, srcs, number, last = bursts[u]
+            for i in rows:
+                s0, s1 = places_of(u, i)
+                if s0 == s1:
+                    continue
+                qv = qvp.tile([P, GROUP, DX_VEC, CB], F32, name="qv")
+                for s in range(s0, s1):
+                    dy = srcs[s] - i + PAD
+                    nc.vector.tensor_tensor(
+                        out=qv[:, s].rearrange("p d (h c) -> p d h c", c=SP),
+                        in0=x3_vector[u][:, s, :]
+                        .rearrange("p (h c) -> p h c", c=SP)
+                        .unsqueeze(1)
+                        .to_broadcast([P, DX_VEC, HEADS, SP]),
+                        in1=weight_tiles[n][:, KW * dy : KW * dy + DX_VEC, :, i % ROWS]
+                        .unsqueeze(3)
+                        .to_broadcast([P, DX_VEC, HEADS, SP]),
+                        op=ALU.mult,
+                    )
+                prod_vector[u, i] = qv
+            for i in rows:
+                s0, s1 = places_of(u, i)
+                if s0 == s1:
+                    continue
+                column = prod_vector[u, i][:, :, DX_VEC - 1, :]
+                if number >= SUM_VEC:
+                    direct_vector.add((u, i))
+                elif (blk, i) in sum_vector:
+                    total, first = sum_vector[blk, i]
+                    if total is None and s1 - s0 < GROUP:
+                        direct_vector.add((u, i))
+                    elif total is None:
+                        total = svp.tile([P, GROUP, CB], F32, name="sv")
+                        sum_vector[blk, i] = (total, None)
+                        nc.gpsimd.tensor_tensor(out=total[:], in0=first, in1=column, op=ALU.add)
+                    else:
+                        nc.gpsimd.tensor_tensor(
+                            out=total[:, s0:s1], in0=total[:, s0:s1], in1=column[:, s0:s1], op=ALU.add
+                        )
+                elif s1 - s0 == GROUP and number + 1 < SUM_VEC:
+                    sum_vector[blk, i] = (None, column)
+                else:
+                    direct_vector.add((u, i))
 
         def scalar_part(u):
-            n, blk, rows, srcs, last = bursts[u]
-            for s, i, dy in readers(u):
-                qa = qap.tile([P, DX_SCA, CB], F32, name="qa")
-                q = i % ROWS
-                for d in range(DX_SCA):
-                    for h in range(HEADS):
-                        nc.scalar.activation(
-                            out=qa[:, d, SP * h : SP * h + SP],
-                            in_=ring[:, slot(srcs[s]), SP * h : SP * h + SP],
-                            func=ACTF.Copy,
-                            scale=weight_tiles[n][:, KW * dy + DX_VEC + d, h, q : q + 1],
-                        )
-                prod_scalar[u, s, i] = qa
-
-        def gpsimd_part(u):
-            n, blk, rows, srcs, last = bursts[u]
-            w5 = weight_tiles[n][:].rearrange("p (y d) h q -> p y d h q", d=KW)
-            additions = []
-
-            def multiply(i, places, tile):
-                s0 = places[0]
-                m = len(places)
-                dy = srcs[s0] - i + PAD
-                nc.gpsimd.tensor_tensor(
-                    out=tile[:, s0 : s0 + m, :].rearrange("p s (h c) -> p s h c", c=SP),
-                    in0=ring[:, slot(srcs[s0]) : slot(srcs[s0]) + m, :].rearrange("p s (h c) -> p s h c", c=SP),
-                    in1=w5[:, dy : dy + m, DX_GPS, :, i % ROWS].unsqueeze(3).to_broadcast([P, m, HEADS, SP]),
-                    op=ALU.mult,
-                )
-
+            n, blk, rows, srcs, number, last = bursts[u]
             for i in rows:
-                places = [s for s, row, dy in readers(u) if row == i]
-                if (blk, i) not in sums:
-                    total = gsp.tile([P, GROUP, CB], F32, name="gs")
-                    sums[blk, i] = (total, set())
-                total, filled = sums[blk, i]
-                handed = []
-                if last:
-                    handed = [(total, s) for s in sorted(filled)]
-                    if len(places) > 0:
-                        qg = qgp.tile([P, GROUP, CB], F32, name="qg")
-                        multiply(i, places, qg)
-                        handed = handed + [(qg, s) for s in places]
+                s0, s1 = places_of(u, i)
+                if s0 == s1:
+                    continue
+                starts = (blk, i) not in sum_scalar and s1 - s0 == GROUP
+                if starts:
+                    qs = ssp.tile([P, GROUP, DX_SCA, CB], F32, name="ss")
+                    sum_scalar[blk, i] = qs
                 else:
-                    fresh = [s for s in places if s not in filled]
-                    old = [s for s in places if s in filled]
-                    if len(old) > 0:
-                        qg = qgp.tile([P, GROUP, CB], F32, name="qg")
-                        multiply(i, old, qg)
-                        additions.append((total, qg, old))
-                    if len(fresh) > 0:
-                        multiply(i, fresh, total)
-                        for s in fresh:
-                            filled.add(s)
-                prod_gpsimd[u, i] = handed
-            for total, qg, places in additions:
-                s0 = places[0]
-                s1 = s0 + len(places)
-                nc.gpsimd.tensor_tensor(
-                    out=total[:, s0:s1, :], in0=total[:, s0:s1, :], in1=qg[:, s0:s1, :], op=ALU.add
-                )
+                    qs = qsp.tile([P, GROUP, DX_SCA, CB], F32, name="qs")
+                for s in range(s0, s1):
+                    dy = srcs[s] - i + PAD
+                    for d in range(DX_SCA):
+                        for h in range(HEADS):
+                            nc.scalar.activation(
+                                out=qs[:, s, d, SP * h : SP * h + SP],
+                                in_=ring[:, slot(srcs[s]), SP * h : SP * h + SP],
+                                func=ACTF.Copy,
+                                scale=weight_tiles[n][:, KW * dy + DX_VEC + d, h, i % ROWS : i % ROWS + 1],
+                            )
+                if starts:
+                    pass
+                elif (blk, i) in sum_scalar:
+                    total = sum_scalar[blk, i]
+                    nc.gpsimd.tensor_tensor(out=total[:, s0:s1], in0=total[:, s0:s1], in1=qs[:, s0:s1], op=ALU.add)
+                else:
+                    direct_scalar.add((u, i))
+                    prod_scalar[u, i] = qs
+            if last:
+                for i in rows:
+                    total = sum_scalar[blk, i]
+                    nc.gpsimd.tensor_tensor(out=total[:, 0], in0=total[:, 0], in1=total[:, 1], op=ALU.add)
 
         def add_up(u):
-            n, blk, rows, srcs, last = bursts[u]
-            for i in rows:
-                places = [s for s, row, dy in readers(u) if row == i]
-                terms = []
-                for s in places:
-                    for d in range(DX_SCA):
-                        terms.append((DX_VEC + d, prod_scalar[u, s, i][:, d, :]))
-                for tile, s in prod_gpsimd[u, i]:
-                    terms.append((DX_GPS, tile[:, s, :]))
-                for s in places:
-                    for dx in range(DX_VEC):
-                        terms.append((dx, prod_vector[u, s, i][:, dx, :]))
+            n, blk, rows, srcs, number, last = bursts[u]
+
+            def transposes(i, terms, closes):
                 for t in range(NT):
                     opens = (blk, i, t) not in accs
                     if opens:
@@ -411,22 +449,46 @@ def tile_sam_pb_t_kernel(tc, logits, x, w3c, b3c, out):
                             lhsT=term[:, P * t : P * t + P],
                             rhs=perm[:, P + shift : 2 * P + shift],
                             start=(opens and m == 0),
-                            stop=(last and m == len(terms) - 1),
+                            stop=(closes and m == len(terms) - 1),
                             is_transpose=True,
                         )
 
+            if u + 2 < nb:
+                x3_for_vector(u + 2)
+            if u + 3 < nb:
+                x3_for_ring(u + 3)
+            for i in rows:
+                s0, s1 = places_of(u, i)
+                terms = []
+                for s in range(s0, s1):
+                    if (u, i) in direct_scalar:
+                        for d in range(DX_SCA):
+                            terms.append((DX_VEC + d, prod_scalar[u, i][:, s, d, :]))
+                    for dx in range(DX_VEC - 1):
+                        terms.append((dx, prod_vector[u, i][:, s, dx, :]))
+                    if (u, i) in direct_vector:
+                        terms.append((DX_VEC - 1, prod_vector[u, i][:, s, DX_VEC - 1, :]))
+                if last:
+                    if (blk, i) in sum_vector:
+                        total, first = sum_vector[blk, i]
+                        for s in range(GROUP):
+                            terms.append((DX_VEC - 1, (first if total is None else total)[:, s, :]))
+                    for d in range(DX_SCA):
+                        terms.append((DX_VEC + d, sum_scalar[blk, i][:, 0, d, :]))
+                transposes(i, terms, last)
+
         def finish(u):
-            n, blk, rows, srcs, last = bursts[u]
+            n, blk, rows, srcs, number, last = bursts[u]
             if not last:
                 return
             for i in rows:
                 if i % STORE == 0:
                     osb = outp.tile([P, NT, NB, STORE, SIDE], F32, name="osb")
-                    stores[0] = osb
+                    store["rows"] = osb
                 for t in range(NT):
                     g = NT * blk + t
                     nc.scalar.activation(
-                        out=stores[0][:, t, :, i % STORE, :],
+                        out=store["rows"][:, t, :, i % STORE, :],
                         in_=accs[blk, i, t][:, 0:P].rearrange("o (j b) -> o b j", b=NB),
                         func=ACTF.Identity,
                         bias=bias_sb[:, g : g + 1],
@@ -437,16 +499,16 @@ def tile_sam_pb_t_kernel(tc, logits, x, w3c, b3c, out):
                         g = NT * blk + t
                         nc.sync.dma_start(
                             out=out[:, P * g : P * g + P, i - STORE + 1 : i + 1, :].rearrange("b o q j -> o b (q j)"),
-                            in_=stores[0][:, t].rearrange("o b q j -> o b (q j)"),
+                            in_=store["rows"][:, t].rearrange("o b q j -> o b (q j)"),
                         )
 
         x3_for_vector(0)
         x3_for_vector(1)
         for v in range(3):
             x3_for_ring(v)
+            copy_ring()
         for v in range(2):
             scalar_part(v)
-            gpsimd_part(v)
         vector_part(0)
         done = 0
         first = 0
@@ -454,22 +516,23 @@ def tile_sam_pb_t_kernel(tc, logits, x, w3c, b3c, out):
             n = bursts[u][0]
             if u > 0:
                 finish(u - 1)
-            if u + 2 < nb:
-                x3_for_vector(u + 2)
-            if u + 3 < nb:
-                x3_for_ring(u + 3)
-            if u + 2 < nb:
-                scalar_part(u + 2)
-                gpsimd_part(u + 2)
+            copy_weights()
             if u + 1 < nb:
                 vector_part(u + 1)
+            if u + 2 < nb:
+                scalar_part(u + 2)
             add_up(u)
+            copy_ring()
             if u > 0 and n != bursts[u - 1][0]:
                 done = 0
                 first = u
             if n + 1 < len(chunks):
-                share = min(len(steps), len(steps) * (u - first + 1) // (chunk_bursts[n] - 3))
-                for step, k in steps[done:share]:
-                    step(n + 1, k)
+                spread = chunk_bursts[n] - 2 - len(weight_steps)
+                share = min(len(softmax_steps), len(softmax_steps) * (u - first + 1) // spread)
+                for step, half, k in softmax_steps[done:share]:
+                    step(n + 1, half, k)
                 done = share
+                if spread <= u - first < spread + len(weight_steps):
+                    step, half, k = weight_steps[u - first - spread]
+                    step(n + 1, half, k)
         finish(nb - 1)

@@ -34,12 +34,13 @@ GROUP = BANK // CB
 ROWS = P // HEADS
 NCHUNK = SIDE // ROWS
 RING = 12
-STORE = 4
+STORE = 2
 
 DX_VEC = 5
 DX_SCA = KW - DX_VEC
-SUM_VEC = 3
+SUM_VEC = 2
 
+WAIT = 6
 REPEAT = 2
 
 FLOPS = 2 * NB * COUT * CIN * SIDE * SIDE + 2 * NB * COUT * SIDE * SIDE * KK
@@ -196,9 +197,13 @@ def tile_sam_pb_t_kernel(tc, logits, x, w3c, b3c, out):
                             out=w5[:, dym, :, :, q], in0=w5[:, dym, :, :, q], in1=w5[:, dy, :, :, q], op=ALU.add
                         )
 
+        def pause(n, half, k):
+            pass
+
         softmax_steps = [(column_maximum, half, b) for half in range(2) for b in range(NB)]
         for half in range(2):
             softmax_steps = softmax_steps + [(exponentials, half, k) for k in range(2 * NB)]
+            softmax_steps = softmax_steps + [(pause, half, 0)] * WAIT
             softmax_steps = softmax_steps + [(reciprocal_sums, half, 0)] + [(normalise, half, dy) for dy in range(KW)]
         weight_steps = [(fold_mirrored_columns, 0, 0)] + [(transpose_weights, 0, k) for k in range(13)]
         weight_steps = weight_steps + [(fold_mirrored_rows, 0, 0)]
@@ -279,7 +284,7 @@ def tile_sam_pb_t_kernel(tc, logits, x, w3c, b3c, out):
 
         ringp = ctx.enter_context(tc.tile_pool(name="ringp", bufs=1))
         qvp = ctx.enter_context(tc.tile_pool(name="qvp", bufs=5))
-        qsp = ctx.enter_context(tc.tile_pool(name="qsp", bufs=3))
+        qsp = ctx.enter_context(tc.tile_pool(name="qsp", bufs=4))
         ssp = ctx.enter_context(tc.tile_pool(name="ssp", bufs=4))
         svp = ctx.enter_context(tc.tile_pool(name="svp", bufs=3))
         outp = ctx.enter_context(tc.tile_pool(name="outp", bufs=2))

@@ -23,6 +23,10 @@ KW = 7
 PAD = KW // 2
 KK = KW * KW
 WIDE = SIDE + 2 * PAD
+NPART = 8
+PCOLS = SIDE // NPART
+EXP_STEP = 8
+NSTEP = NB * PCOLS // EXP_STEP
 HALF = SIDE // 2
 
 BANK = 512
@@ -34,13 +38,16 @@ GROUP = BANK // CB
 ROWS = P // HEADS
 NCHUNK = SIDE // ROWS
 RING = 12
-STORE = 2
 
 DX_VEC = 5
 DX_SCA = KW - DX_VEC
 SUM_VEC = 2
 
-WAIT = 6
+EXP_BURSTS = 12
+FIRST_EXP = 3
+LEAD = 3
+MAX_BURSTS = 8
+
 REPEAT = 2
 
 FLOPS = 2 * NB * COUT * CIN * SIDE * SIDE + 2 * NB * COUT * SIDE * SIDE * KK
@@ -88,8 +95,8 @@ def tile_sam_pb_t_kernel(tc, logits, x, w3c, b3c, out):
         def load_logits(n):
             blk, ic = chunks[n]
             lg = soft.tile([P, NB, KK, SIDE], BF16, name="lg")
-            for h in range(HEADS):
-                for b in range(NB):
+            for b in range(NB):
+                for h in range(HEADS):
                     nc.sync.dma_start(
                         out=lg[ROWS * h : ROWS * h + ROWS, b],
                         in_=logits[b, HEADS * blk + h, :, SIDE * ROWS * ic : SIDE * ROWS * (ic + 1)].rearrange(
@@ -102,8 +109,6 @@ def tile_sam_pb_t_kernel(tc, logits, x, w3c, b3c, out):
             if half == 0 and b == 0:
                 cur["max"] = soft.tile([P, NB, SIDE], F32, name="mx")
                 cur["neg"] = soft.tile([P, NB, SIDE], F32, name="ng")
-                cur["sum"] = soft.tile([P, NB, SIDE], F32, name="sm")
-                cur["inv"] = soft.tile([P, NB, SIDE], F32, name="rs")
             j0 = HALF * half
             nc.vector.tensor_reduce(
                 out=cur["max"][:, b, j0 : j0 + HALF],
@@ -111,58 +116,72 @@ def tile_sam_pb_t_kernel(tc, logits, x, w3c, b3c, out):
                 axis=AX.X,
                 op=ALU.max,
             )
+
+        def negate_maximum(b0, b1, j0, j1):
             nc.vector.tensor_scalar_mul(
-                out=cur["neg"][:, b, j0 : j0 + HALF], in0=cur["max"][:, b, j0 : j0 + HALF], scalar1=-1.0
+                out=cur["neg"][:, b0:b1, j0:j1], in0=cur["max"][:, b0:b1, j0:j1], scalar1=-1.0
             )
 
-        def exponentials(n, half, k, pool=soft):
+        def maximum_step(n, half, b):
+            column_maximum(n, half, b)
+            if b == NB - 1:
+                negate_maximum(0, NB, HALF * half, HALF * half + HALF)
+
+        def open_softmax(n):
+            cur["sum"] = soft.tile([P, NPART, NB, PCOLS], F32, name="sm")
+            cur["inv"] = soft.tile([P, NPART, NB, PCOLS], F32, name="rs")
+
+        def exponential(n, part, b, m):
+            j = PCOLS * part + m
+            nc.scalar.activation(
+                out=cur["exp", part][:, b, m, :],
+                in_=logit_tiles[n][:, b, :, j],
+                func=ACTF.Exp,
+                bias=cur["neg"][:, b, j : j + 1],
+                scale=1.0,
+                accum_out=cur["sum"][:, part, b, m : m + 1],
+            )
+
+        def exponentials(n, part, k):
+            if part == 0 and k == 0:
+                open_softmax(n)
             if k == 0:
-                cur["exp", half] = pool.tile([P, NB, HALF, KK], F32, name="ex")
-            b = k // 2
-            for m in range(8 * (k % 2), 8 * (k % 2) + 8):
-                j = HALF * half + m
-                nc.scalar.activation(
-                    out=cur["exp", half][:, b, m, :],
-                    in_=logit_tiles[n][:, b, :, j],
-                    func=ACTF.Exp,
-                    bias=cur["neg"][:, b, j : j + 1],
-                    scale=1.0,
-                    accum_out=cur["sum"][:, b, j : j + 1],
-                )
+                cur["exp", part] = soft.tile([P, NB, PCOLS, KK], F32, name="ex", bufs=4)
+            for e in range(EXP_STEP * k, EXP_STEP * k + EXP_STEP):
+                exponential(n, part, e // PCOLS, e % PCOLS)
 
-        def reciprocal_sums(n, half, k):
-            j0 = HALF * half
-            nc.vector.reciprocal(out=cur["inv"][:, :, j0 : j0 + HALF], in_=cur["sum"][:, :, j0 : j0 + HALF])
-            if half == 1 and n + 1 < len(chunks):
-                load_logits(n + 1)
+        def reciprocal_sums(n, part, k):
+            nc.vector.reciprocal(out=cur["inv"][:, part], in_=cur["sum"][:, part])
 
-        def normalise(n, half, dy):
-            j0 = HALF * half
-            nc.vector.tensor_tensor(
-                out=wpad[:, KW * dy : KW * dy + KW, PAD + j0 : PAD + j0 + HALF, :],
-                in0=cur["exp", half][:, :, :, KW * dy : KW * dy + KW].rearrange("p b j l -> p l j b"),
-                in1=cur["inv"][:, :, j0 : j0 + HALF]
+        def normalise(n, part, k):
+            engine = nc.vector if n == 0 else nc.gpsimd
+            j0 = PAD + PCOLS * part
+            engine.tensor_tensor(
+                out=wpad[:, :, j0 : j0 + PCOLS, :],
+                in0=cur["exp", part][:].rearrange("p b j l -> p l j b"),
+                in1=cur["inv"][:, part]
                 .rearrange("p b j -> p j b")
                 .unsqueeze(1)
-                .to_broadcast([P, KW, HALF, NB]),
+                .to_broadcast([P, KK, PCOLS, NB]),
                 op=ALU.mult,
             )
 
-        def fold_mirrored_columns(n, half, k):
+        def fold_mirrored_columns(n, part, k):
+            engine = nc.vector if n == 0 else nc.gpsimd
             w5 = wpad[:].rearrange("p (y d) j b -> p y d j b", d=KW)
             for j in list(range(PAD)) + list(range(SIDE - PAD, SIDE)):
                 for dx in range(KW):
                     c = j + dx - PAD
                     if c != reflect(c):
                         dxm = reflect(c) - j + PAD
-                        nc.vector.tensor_tensor(
+                        engine.tensor_tensor(
                             out=w5[:, :, dxm, PAD + j, :],
                             in0=w5[:, :, dxm, PAD + j, :],
                             in1=w5[:, :, dx, PAD + j, :],
                             op=ALU.add,
                         )
 
-        def transpose_weights(n, half, k):
+        def transpose_weights(n, part, k):
             if k == 0:
                 weight_tiles.append(wsp.tile([P, KK, HEADS, ROWS], F32, name="ws"))
             flat = wpad[:].rearrange("p l j b -> p l (j b)")
@@ -184,7 +203,8 @@ def tile_sam_pb_t_kernel(tc, logits, x, w3c, b3c, out):
                 )
             transposed.clear()
 
-        def fold_mirrored_rows(n, half, k):
+        def fold_mirrored_rows(n, part, k):
+            engine = nc.vector if n == 0 else nc.gpsimd
             ic = chunks[n][1]
             w5 = weight_tiles[n][:].rearrange("p (y d) h q -> p y d h q", d=KW)
             for q in range(ROWS):
@@ -193,101 +213,40 @@ def tile_sam_pb_t_kernel(tc, logits, x, w3c, b3c, out):
                     a = i + dy - PAD
                     if a != reflect(a):
                         dym = reflect(a) - i + PAD
-                        nc.vector.tensor_tensor(
+                        engine.tensor_tensor(
                             out=w5[:, dym, :, :, q], in0=w5[:, dym, :, :, q], in1=w5[:, dy, :, :, q], op=ALU.add
                         )
 
-        def pause(n, half, k):
-            pass
+        def logits_step(n, part, k):
+            load_logits(n)
 
-        softmax_steps = [(column_maximum, half, b) for half in range(2) for b in range(NB)]
-        for half in range(2):
-            softmax_steps = softmax_steps + [(exponentials, half, k) for k in range(2 * NB)]
-            softmax_steps = softmax_steps + [(pause, half, 0)] * WAIT
-            softmax_steps = softmax_steps + [(reciprocal_sums, half, 0)] + [(normalise, half, dy) for dy in range(KW)]
-        weight_steps = [(fold_mirrored_columns, 0, 0)] + [(transpose_weights, 0, k) for k in range(13)]
-        weight_steps = weight_steps + [(fold_mirrored_rows, 0, 0)]
+        weight_steps = [(fold_mirrored_columns, 0)] + [(transpose_weights, k) for k in range((KK + 3) // 4)]
+        weight_steps = weight_steps + [(fold_mirrored_rows, 0)]
 
-        make_identity(nc, ident_bf[:])
-        make_identity(nc, perm[:, 0:P])
-        nc.gpsimd.memset(wpad[:], 0.0)
-
-        with tc.tile_pool(name="stage", bufs=1) as stage:
-            w_sb = stage.tile([P, COUT // P, CIN], BF16)
-            nc.sync.dma_start(out=w_sb[:], in_=w3c.rearrange("(g p) c -> p g c", p=P))
-            XP = 256
-            x_sb = stage.tile([P, 4, NB, PACK, XP], BF16)
-            for part in range(4):
-                for b in range(NB):
-                    nc.scalar.dma_start(
-                        out=x_sb[:, part, b],
-                        in_=x[b].rearrange("(p t) i j -> p t (i j)", t=PACK)[:, :, XP * part : XP * part + XP],
-                    )
-            load_logits(0)
-            b_rows = stage.tile([P, P], BF16)
-            nc.vector.memset(b_rows[:], 0.0)
-            nc.scalar.dma_start(out=b_rows[0 : COUT // P, :], in_=b3c.rearrange("(g o) -> g o", g=COUT // P))
-            nc.vector.tensor_copy(out=perm[:, P : 2 * P], in_=perm[:, 0:P])
-            nc.vector.tensor_copy(out=perm[:, 2 * P : 3 * P], in_=perm[:, 0:P])
-
-            w_grp = stage.tile([P, COUT // P, P, PACK], BF16, align_bytes=64)
-            for g in range(COUT // P):
-                wtb = psacc.tile([P, PACK, P], BF16, name="acc")
-                for t in range(PACK):
-                    nc.tensor.transpose(wtb[:, t, :], w_sb[:, g, t:CIN:PACK], ident_bf[:])
-                nc.scalar.copy(out=w_grp[:, g], in_=wtb[:].rearrange("p t o -> p o t"))
-            btp = pswt.tile([P, P], BF16, name="wt")
-            nc.tensor.transpose(btp[:], b_rows[:], ident_bf[:])
-
-            x_parts = []
-
-            def interleave(part):
-                xg = stage.tile([P, XP, NB, PACK], BF16, align_bytes=64, name="xg", bufs=2)
-                for b in range(NB):
-                    nc.vector.tensor_copy(out=xg[:, :, b, :], in_=x_sb[:, part, b].rearrange("p t n -> p n t"))
-                x_parts.append(xg)
-
-            def quantise(part):
-                n0 = XP * NB * part
-                nc.vector.quantize_mx(
-                    out=xq[:, n0 : n0 + XP * NB].bitcast(FP8X4),
-                    scales=xs[:, n0 : n0 + XP * NB],
-                    in_=x_parts[part][:].rearrange("p n b t -> p (n b t)"),
-                )
-
-            interleave(0)
-            for part in range(4):
-                if part + 1 < 4:
-                    interleave(part + 1)
-                quantise(part)
-            nc.vector.quantize_mx(
-                out=wq[:].bitcast(FP8X4),
-                scales=wsc[:],
-                in_=w_grp[:].rearrange("p g o t -> p (g o t)"),
-            )
-            nc.vector.tensor_copy(out=bias_sb[:], in_=btp[:, 0 : COUT // P])
-
-            for half in range(2):
-                for b in range(NB):
-                    column_maximum(0, half, b)
-            for half in range(2):
+        def make_plan(n, length):
+            plan = [[] for r in range(length)]
+            if n + 1 < len(chunks):
+                first = FIRST_EXP if n == 0 else 0
+                if n == 0:
+                    for k in range(2 * NB):
+                        plan[first - 2 + k // NB].append((maximum_step, n + 1, k // NB, k % NB))
+                for part in range(NPART):
+                    for k in range(NSTEP):
+                        r = first + (NSTEP * part + k) * (EXP_BURSTS - first) // (NSTEP * NPART)
+                        plan[r].append((exponentials, n + 1, part, k))
+                    plan[r + 1].append((reciprocal_sums, n + 1, part, 0))
+                    plan[r + 2].append((normalise, n + 1, part, 0))
+                start = length - LEAD - len(weight_steps)
+                assert r + 2 <= start
+                for k, (step, arg) in enumerate(weight_steps):
+                    plan[start + k].append((step, n + 1, 0, arg))
+            if n + 2 < len(chunks):
+                plan[EXP_BURSTS].append((logits_step, n + 2, 0, 0))
                 for k in range(2 * NB):
-                    exponentials(0, half, k, soft if half == 0 else stage)
-                reciprocal_sums(0, half, 0)
-                for dy in range(KW):
-                    normalise(0, half, dy)
-            fold_mirrored_columns(0, 0, 0)
-            for k in range(13):
-                transpose_weights(0, 0, k)
-                copy_weights()
-            fold_mirrored_rows(0, 0, 0)
+                    plan[length - 1 - MAX_BURSTS + k].append((maximum_step, n + 2, k // NB, k % NB))
+            return plan
 
         ringp = ctx.enter_context(tc.tile_pool(name="ringp", bufs=1))
-        qvp = ctx.enter_context(tc.tile_pool(name="qvp", bufs=5))
-        qsp = ctx.enter_context(tc.tile_pool(name="qsp", bufs=4))
-        ssp = ctx.enter_context(tc.tile_pool(name="ssp", bufs=4))
-        svp = ctx.enter_context(tc.tile_pool(name="svp", bufs=3))
-        outp = ctx.enter_context(tc.tile_pool(name="outp", bufs=2))
 
         bursts = []
         chunk_bursts = []
@@ -358,6 +317,108 @@ def tile_sam_pb_t_kernel(tc, logits, x, w3c, b3c, out):
                 nc.scalar.copy(out=ring[:, s0 : s0 + len(new), :], in_=xb[:, 0 : len(new), :])
             ring_copies.clear()
 
+        make_identity(nc, ident_bf[:])
+        make_identity(nc, perm[:, 0:P])
+        nc.gpsimd.memset(wpad[:], 0.0)
+
+        with tc.tile_pool(name="stage", bufs=1) as stage:
+            w_sb = stage.tile([P, COUT // P, CIN], BF16)
+            nc.scalar.dma_start(out=w_sb[:], in_=w3c.rearrange("(g p) c -> p g c", p=P))
+            b_rows = stage.tile([P, P], BF16)
+            nc.vector.memset(b_rows[:], 0.0)
+            nc.scalar.dma_start(out=b_rows[0 : COUT // P, :], in_=b3c.rearrange("(g o) -> g o", g=COUT // P))
+            XP = 256
+            x_sb = stage.tile([P, 4, NB, PACK, XP], BF16)
+
+            def load_x(queue, part):
+                for b in range(NB):
+                    queue.dma_start(
+                        out=x_sb[:, part, b],
+                        in_=x[b].rearrange("(p t) i j -> p t (i j)", t=PACK)[:, :, XP * part : XP * part + XP],
+                    )
+
+            load_logits(0)
+            load_x(nc.scalar, 0)
+            load_x(nc.scalar, 1)
+            load_x(nc.sync, 2)
+            load_x(nc.sync, 3)
+            nc.vector.tensor_copy(out=perm[:, P : 2 * P], in_=perm[:, 0:P])
+            nc.vector.tensor_copy(out=perm[:, 2 * P : 3 * P], in_=perm[:, 0:P])
+
+            w_grp = stage.tile([P, COUT // P, P, PACK], BF16, align_bytes=64)
+            for g in range(COUT // P):
+                wtb = psacc.tile([P, PACK, P], BF16, name="acc")
+                for t in range(PACK):
+                    nc.tensor.transpose(wtb[:, t, :], w_sb[:, g, t:CIN:PACK], ident_bf[:])
+                nc.scalar.copy(out=w_grp[:, g], in_=wtb[:].rearrange("p t o -> p o t"))
+            btp = pswt.tile([P, P], BF16, name="wt")
+            nc.tensor.transpose(btp[:], b_rows[:], ident_bf[:])
+
+            x_parts = []
+
+            def interleave(part, b0, b1, copy):
+                if b0 == 0:
+                    xg = stage.tile([P, XP, NB, PACK], BF16, align_bytes=64, name="xg", bufs=2)
+                    x_parts.append(xg)
+                for b in range(b0, b1):
+                    copy(out=x_parts[part][:, :, b, :], in_=x_sb[:, part, b].rearrange("p t n -> p n t"))
+
+            def quantise(part):
+                n0 = XP * NB * part
+                nc.vector.quantize_mx(
+                    out=xq[:, n0 : n0 + XP * NB].bitcast(FP8X4),
+                    scales=xs[:, n0 : n0 + XP * NB],
+                    in_=x_parts[part][:].rearrange("p n b t -> p (n b t)"),
+                )
+
+            open_softmax(0)
+            exp_first = stage.tile([P, NPART, NB, PCOLS, KK], F32)
+            for part in range(NPART):
+                cur["exp", part] = exp_first[:, part]
+
+            interleave(0, 0, NB, nc.vector.tensor_copy)
+            quantise(0)
+            for b in range(NB):
+                for half in range(2):
+                    column_maximum(0, half, b)
+                negate_maximum(b, b + 1, 0, SIDE)
+                if b == 0:
+                    nc.vector.quantize_mx(
+                        out=wq[:].bitcast(FP8X4),
+                        scales=wsc[:],
+                        in_=w_grp[:].rearrange("p g o t -> p (g o t)"),
+                    )
+                    nc.vector.tensor_copy(out=bias_sb[:], in_=btp[:, 0 : COUT // P])
+                elif b < 3:
+                    interleave(1, 2 * b - 2, 2 * b, nc.vector.tensor_copy)
+                for part in range(NPART):
+                    for m in range(PCOLS):
+                        exponential(0, part, b, m)
+            quantise(1)
+            for part in range(NPART):
+                reciprocal_sums(0, part, 0)
+                normalise(0, part, 0)
+            for v in range(2):
+                x3_for_vector(v)
+            for v in range(3):
+                x3_for_ring(v)
+                copy_ring()
+            load_logits(1)
+            fold_mirrored_columns(0, 0, 0)
+            interleave(2, 0, NB, nc.scalar.copy)
+            interleave(3, 0, NB, nc.vector.tensor_copy)
+            quantise(2)
+            quantise(3)
+            for step, k in weight_steps[1:]:
+                step(0, 0, k)
+                copy_weights()
+
+        qvp = ctx.enter_context(tc.tile_pool(name="qvp", bufs=5))
+        qsp = ctx.enter_context(tc.tile_pool(name="qsp", bufs=4))
+        ssp = ctx.enter_context(tc.tile_pool(name="ssp", bufs=4))
+        svp = ctx.enter_context(tc.tile_pool(name="svp", bufs=3))
+        outp = ctx.enter_context(tc.tile_pool(name="outp", bufs=2))
+
         def vector_part(u):
             n, blk, rows, srcs, number, last = bursts[u]
             for i in rows:
@@ -403,9 +464,11 @@ def tile_sam_pb_t_kernel(tc, logits, x, w3c, b3c, out):
                 else:
                     direct_vector.add((u, i))
 
-        def scalar_part(u):
+        def scalar_part(u, between):
             n, blk, rows, srcs, number, last = bursts[u]
             for i in rows:
+                if i == rows[1]:
+                    between()
                 s0, s1 = places_of(u, i)
                 if s0 == s1:
                     continue
@@ -482,62 +545,54 @@ def tile_sam_pb_t_kernel(tc, logits, x, w3c, b3c, out):
                         terms.append((DX_VEC + d, sum_scalar[blk, i][:, 0, d, :]))
                 transposes(i, terms, last)
 
-        def finish(u):
+        def finish(u, r):
             n, blk, rows, srcs, number, last = bursts[u]
             if not last:
                 return
-            for i in rows:
-                if i % STORE == 0:
-                    osb = outp.tile([P, NT, NB, STORE, SIDE], F32, name="osb")
-                    store["rows"] = osb
+            i = rows[r]
+            if r == 0:
+                store["rows"] = outp.tile([P, NT, NB, GROUP, SIDE], F32, name="osb")
+            for t in range(NT):
+                g = NT * blk + t
+                nc.scalar.activation(
+                    out=store["rows"][:, t, :, r, :],
+                    in_=accs[blk, i, t][:, 0:P].rearrange("o (j b) -> o b j", b=NB),
+                    func=ACTF.Identity,
+                    bias=bias_sb[:, g : g + 1],
+                    scale=1.0,
+                )
+            if r == GROUP - 1:
                 for t in range(NT):
                     g = NT * blk + t
-                    nc.scalar.activation(
-                        out=store["rows"][:, t, :, i % STORE, :],
-                        in_=accs[blk, i, t][:, 0:P].rearrange("o (j b) -> o b j", b=NB),
-                        func=ACTF.Identity,
-                        bias=bias_sb[:, g : g + 1],
-                        scale=1.0,
+                    nc.sync.dma_start(
+                        out=out[:, P * g : P * g + P, rows[0] : i + 1, :].rearrange("b o q j -> o b (q j)"),
+                        in_=store["rows"][:, t].rearrange("o b q j -> o b (q j)"),
                     )
-                if i % STORE == STORE - 1:
-                    for t in range(NT):
-                        g = NT * blk + t
-                        nc.sync.dma_start(
-                            out=out[:, P * g : P * g + P, i - STORE + 1 : i + 1, :].rearrange("b o q j -> o b (q j)"),
-                            in_=store["rows"][:, t].rearrange("o b q j -> o b (q j)"),
-                        )
 
-        x3_for_vector(0)
-        x3_for_vector(1)
-        for v in range(3):
-            x3_for_ring(v)
-            copy_ring()
-        for v in range(2):
-            scalar_part(v)
         vector_part(0)
-        done = 0
-        first = 0
+        for v in range(2):
+            scalar_part(v, lambda: None)
+        plan = []
+        for n, length in enumerate(chunk_bursts):
+            plan.extend(make_plan(n, length))
         for u in range(nb):
-            n = bursts[u][0]
+
+            def between():
+                if u > 0:
+                    finish(u - 1, 1)
+                copy_weights()
+
             if u > 0:
-                finish(u - 1)
-            copy_weights()
+                finish(u - 1, 0)
             if u + 1 < nb:
                 vector_part(u + 1)
             if u + 2 < nb:
-                scalar_part(u + 2)
+                scalar_part(u + 2, between)
+            else:
+                between()
             add_up(u)
             copy_ring()
-            if u > 0 and n != bursts[u - 1][0]:
-                done = 0
-                first = u
-            if n + 1 < len(chunks):
-                spread = chunk_bursts[n] - 2 - len(weight_steps)
-                share = min(len(softmax_steps), len(softmax_steps) * (u - first + 1) // spread)
-                for step, half, k in softmax_steps[done:share]:
-                    step(n + 1, half, k)
-                done = share
-                if spread <= u - first < spread + len(weight_steps):
-                    step, half, k = weight_steps[u - first - spread]
-                    step(n + 1, half, k)
-        finish(nb - 1)
+            for step, n, part, k in plan[u]:
+                step(n, part, k)
+        for r in range(GROUP):
+            finish(nb - 1, r)

from contextlib import ExitStack

import concourse.mybir as mybir
from concourse.masks import make_identity

F32 = mybir.dt.float32
BF16 = mybir.dt.bfloat16
U32 = mybir.dt.uint32
U8 = mybir.dt.uint8
FP8X4 = mybir.dt.float8_e4m3fn_x4
ALU = mybir.AluOpType
ACTF = mybir.ActivationFunctionType
AX = mybir.AxisListType

P = 128
NB = 4
CIN = 512
PACK = 4
SIDE = 32
COUT = 1024
SP = 32
KW = 7
PAD = KW // 2
KK = KW * KW
WIDE = SIDE + 2 * PAD
NPART = 8
PCOLS = SIDE // NPART
EXP_STEP = 8
NSTEP = NB * PCOLS // EXP_STEP
HALF = SIDE // 2

BANK = 512
CB = 256
NBLK = COUT // CB
HEADS = CB // SP
NT = CB // P
GROUP = BANK // CB
ROWS = P // HEADS
NCHUNK = SIDE // ROWS
RING = 12

DX_VEC = 5
DX_SCA = KW - DX_VEC
SUM_VEC = 2

EXP_BURSTS = 12
FIRST_EXP = 3
LEAD = 3
MAX_BURSTS = 8

REPEAT = 2

FLOPS = 2 * NB * COUT * CIN * SIDE * SIDE + 2 * NB * COUT * SIDE * SIDE * KK


def reflect(u):
    if u < 0:
        return -u
    if u > SIDE - 1:
        return 2 * (SIDE - 1) - u
    return u


def source_rows(i):
    return sorted(set(reflect(i + dy - PAD) for dy in range(KW)))


def tile_sam_pb_t_kernel(tc, logits, x, w3c, b3c, out):
    nc = tc.nc
    with ExitStack() as ctx:
        ctx.enter_context(tc.manual_schedule())
        const = ctx.enter_context(tc.tile_pool(name="const", bufs=1))
        soft = ctx.enter_context(tc.tile_pool(name="soft", bufs=1))
        wsp = ctx.enter_context(tc.tile_pool(name="wsp", bufs=2))
        psa = ctx.enter_context(tc.psum_pool(name="psa", bufs=2))
        psacc = ctx.enter_context(tc.psum_pool(name="psacc", bufs=4))
        psring = ctx.enter_context(tc.psum_pool(name="psring", bufs=1))
        pswt = ctx.enter_context(tc.psum_pool(name="pswt", bufs=1))

        xq = const.tile([P, SIDE * P], U32, align_bytes=64)
        xs = const.tile([P, SIDE * P], U8, align_bytes=64)
        wq = const.tile([P, COUT], U32, align_bytes=64)
        wsc = const.tile([P, COUT], U8, align_bytes=64)
        perm = const.tile([P, 3 * P], F32)
        ident_bf = const.tile([P, P], BF16)
        bias_sb = const.tile([P, COUT // P], F32)
        wpad = const.tile([P, KK, WIDE, NB], F32)

        chunks = [(blk, ic) for blk in range(NBLK) for ic in range(NCHUNK)]
        logit_tiles = []
        weight_tiles = []
        transposed = []
        cur = {}

        def load_logits(n):
            blk, ic = chunks[n]
            lg = soft.tile([P, NB, KK, SIDE], BF16, name="lg")
            for b in range(NB):
                for h in range(HEADS):
                    nc.sync.dma_start(
                        out=lg[ROWS * h : ROWS * h + ROWS, b],
                        in_=logits[b, HEADS * blk + h, :, SIDE * ROWS * ic : SIDE * ROWS * (ic + 1)].rearrange(
                            "l (q j) -> q l j", q=ROWS
                        ),
                    )
            logit_tiles.append(lg)

        def column_maximum(n, half, b):
            if half == 0 and b == 0:
                cur["max"] = soft.tile([P, NB, SIDE], F32, name="mx")
                cur["neg"] = soft.tile([P, NB, SIDE], F32, name="ng")
            j0 = HALF * half
            nc.vector.tensor_reduce(
                out=cur["max"][:, b, j0 : j0 + HALF],
                in_=logit_tiles[n][:, b, :, j0 : j0 + HALF].rearrange("p l j -> p j l"),
                axis=AX.X,
                op=ALU.max,
            )

        def negate_maximum(b0, b1, j0, j1):
            nc.vector.tensor_scalar_mul(
                out=cur["neg"][:, b0:b1, j0:j1], in0=cur["max"][:, b0:b1, j0:j1], scalar1=-1.0
            )

        def maximum_step(n, half, b):
            column_maximum(n, half, b)
            if b == NB - 1:
                negate_maximum(0, NB, HALF * half, HALF * half + HALF)

        def open_softmax(n):
            cur["sum"] = soft.tile([P, NPART, NB, PCOLS], F32, name="sm")
            cur["inv"] = soft.tile([P, NPART, NB, PCOLS], F32, name="rs")

        def exponential(n, part, b, m):
            j = PCOLS * part + m
            nc.scalar.activation(
                out=cur["exp", part][:, b, m, :],
                in_=logit_tiles[n][:, b, :, j],
                func=ACTF.Exp,
                bias=cur["neg"][:, b, j : j + 1],
                scale=1.0,
                accum_out=cur["sum"][:, part, b, m : m + 1],
            )

        def exponentials(n, part, k):
            if part == 0 and k == 0:
                open_softmax(n)
            if k == 0:
                cur["exp", part] = soft.tile([P, NB, PCOLS, KK], F32, name="ex", bufs=4)
            for e in range(EXP_STEP * k, EXP_STEP * k + EXP_STEP):
                exponential(n, part, e // PCOLS, e % PCOLS)

        def reciprocal_sums(n, part, k):
            nc.vector.reciprocal(out=cur["inv"][:, part], in_=cur["sum"][:, part])

        def normalise(n, part, k):
            engine = nc.vector if n == 0 else nc.gpsimd
            j0 = PAD + PCOLS * part
            engine.tensor_tensor(
                out=wpad[:, :, j0 : j0 + PCOLS, :],
                in0=cur["exp", part][:].rearrange("p b j l -> p l j b"),
                in1=cur["inv"][:, part]
                .rearrange("p b j -> p j b")
                .unsqueeze(1)
                .to_broadcast([P, KK, PCOLS, NB]),
                op=ALU.mult,
            )

        def fold_mirrored_columns(n, part, k):
            engine = nc.vector if n == 0 else nc.gpsimd
            w5 = wpad[:].rearrange("p (y d) j b -> p y d j b", d=KW)
            for j in list(range(PAD)) + list(range(SIDE - PAD, SIDE)):
                for dx in range(KW):
                    c = j + dx - PAD
                    if c != reflect(c):
                        dxm = reflect(c) - j + PAD
                        engine.tensor_tensor(
                            out=w5[:, :, dxm, PAD + j, :],
                            in0=w5[:, :, dxm, PAD + j, :],
                            in1=w5[:, :, dx, PAD + j, :],
                            op=ALU.add,
                        )

        def transpose_weights(n, part, k):
            if k == 0:
                weight_tiles.append(wsp.tile([P, KK, HEADS, ROWS], F32, name="ws"))
            flat = wpad[:].rearrange("p l j b -> p l (j b)")
            l0 = 4 * k
            m = min(4, KK - l0)
            if n == 0:
                wt = psacc.tile([P, 4, P], F32, name="acc")
            else:
                wt = pswt.tile([P, 4, P], F32, name="wt")
            for r in range(m):
                first = NB * (2 * PAD - (l0 + r) % KW)
                nc.tensor.transpose(wt[:, r, :], flat[:, l0 + r, first : first + P], perm[:, P : 2 * P])
            transposed.append((n, l0, m, wt))

        def copy_weights():
            for n, l0, m, wt in transposed:
                nc.scalar.copy(
                    out=weight_tiles[n][:, l0 : l0 + m].rearrange("p l h q -> p l (h q)"), in_=wt[:, 0:m, :]
                )
            transposed.clear()

        def fold_mirrored_rows(n, part, k):
            engine = nc.vector if n == 0 else nc.gpsimd
            ic = chunks[n][1]
            w5 = weight_tiles[n][:].rearrange("p (y d) h q -> p y d h q", d=KW)
            for q in range(ROWS):
                i = ROWS * ic + q
                for dy in range(KW):
                    a = i + dy - PAD
                    if a != reflect(a):
                        dym = reflect(a) - i + PAD
                        engine.tensor_tensor(
                            out=w5[:, dym, :, :, q], in0=w5[:, dym, :, :, q], in1=w5[:, dy, :, :, q], op=ALU.add
                        )

        def logits_step(n, part, k):
            load_logits(n)

        weight_steps = [(fold_mirrored_columns, 0)] + [(transpose_weights, k) for k in range((KK + 3) // 4)]
        weight_steps = weight_steps + [(fold_mirrored_rows, 0)]

        def make_plan(n, length):
            plan = [[] for r in range(length)]
            if n + 1 < len(chunks):
                first = FIRST_EXP if n == 0 else 0
                if n == 0:
                    for k in range(2 * NB):
                        plan[first - 2 + k // NB].append((maximum_step, n + 1, k // NB, k % NB))
                for part in range(NPART):
                    for k in range(NSTEP):
                        r = first + (NSTEP * part + k) * (EXP_BURSTS - first) // (NSTEP * NPART)
                        plan[r].append((exponentials, n + 1, part, k))
                    plan[r + 1].append((reciprocal_sums, n + 1, part, 0))
                    plan[r + 2].append((normalise, n + 1, part, 0))
                start = length - LEAD - len(weight_steps)
                assert r + 2 <= start
                for k, (step, arg) in enumerate(weight_steps):
                    plan[start + k].append((step, n + 1, 0, arg))
            if n + 2 < len(chunks):
                plan[EXP_BURSTS].append((logits_step, n + 2, 0, 0))
                for k in range(2 * NB):
                    plan[length - 1 - MAX_BURSTS + k].append((maximum_step, n + 2, k // NB, k % NB))
            return plan

        ringp = ctx.enter_context(tc.tile_pool(name="ringp", bufs=1))

        bursts = []
        chunk_bursts = []
        for n, (blk, ic) in enumerate(chunks):
            before = len(bursts)
            for q in range(0, ROWS, GROUP):
                rows = [ROWS * ic + q + r for r in range(GROUP)]
                srcs = sorted(set(a for i in rows for a in source_rows(i)))
                for s in range(0, len(srcs), GROUP):
                    bursts.append((n, blk, rows, srcs[s : s + GROUP], s // GROUP, s + GROUP >= len(srcs)))
            chunk_bursts.append(len(bursts) - before)
        nb = len(bursts)

        ring = ringp.tile([P, RING, CB], F32)
        in_ring = set()
        ring_copies = []
        x3_vector = {}
        prod_vector = {}
        prod_scalar = {}
        sum_vector = {}
        sum_scalar = {}
        direct_vector = set()
        direct_scalar = set()
        accs = {}
        store = {}

        def slot(a):
            return (a + 1) % RING

        def places_of(u, i):
            places = [s for s, a in enumerate(bursts[u][3]) if a in source_rows(i)]
            if len(places) == 0:
                return 0, 0
            return places[0], places[-1] + 1

        def x3_passes(blk, srcs, tile):
            for s, a in enumerate(srcs):
                nc.tensor.matmul_mx(
                    out=tile[:, s, :],
                    lhsT=xq[:, P * a : P * a + P].bitcast(FP8X4),
                    lhsT_scale=xs[:, P * a : P * a + P],
                    rhs=wq[:, CB * blk : CB * blk + CB].bitcast(FP8X4),
                    rhs_scale=wsc[:, CB * blk : CB * blk + CB],
                    start=True,
                    stop=True,
                )

        def x3_for_vector(u):
            n, blk, rows, srcs, number, last = bursts[u]
            xa = psa.tile([P, GROUP, CB], F32, name="xa")
            for k in range(REPEAT):
                x3_passes(blk, srcs, xa)
            x3_vector[u] = xa

        def x3_for_ring(u):
            n, blk, rows, srcs, number, last = bursts[u]
            new = [a for a in srcs if (blk, a) not in in_ring]
            if len(new) > 0:
                xb = psring.tile([P, GROUP, CB], F32, name="xb")
                x3_passes(blk, new, xb)
                ring_copies.append((new, xb))
                for a in new:
                    in_ring.add((blk, a))

        def copy_ring():
            for new, xb in ring_copies:
                s0 = slot(new[0])
                nc.scalar.copy(out=ring[:, s0 : s0 + len(new), :], in_=xb[:, 0 : len(new), :])
            ring_copies.clear()

        make_identity(nc, ident_bf[:])
        make_identity(nc, perm[:, 0:P])
        nc.gpsimd.memset(wpad[:], 0.0)

        with tc.tile_pool(name="stage", bufs=1) as stage:
            w_sb = stage.tile([P, COUT // P, CIN], BF16)
            nc.scalar.dma_start(out=w_sb[:], in_=w3c.rearrange("(g p) c -> p g c", p=P))
            b_rows = stage.tile([P, P], BF16)
            nc.vector.memset(b_rows[:], 0.0)
            nc.scalar.dma_start(out=b_rows[0 : COUT // P, :], in_=b3c.rearrange("(g o) -> g o", g=COUT // P))
            XP = 256
            x_sb = stage.tile([P, 4, NB, PACK, XP], BF16)

            def load_x(queue, part):
                for b in range(NB):
                    queue.dma_start(
                        out=x_sb[:, part, b],
                        in_=x[b].rearrange("(p t) i j -> p t (i j)", t=PACK)[:, :, XP * part : XP * part + XP],
                    )

            load_logits(0)
            load_x(nc.scalar, 0)
            load_x(nc.scalar, 1)
            load_x(nc.sync, 2)
            load_x(nc.sync, 3)
            nc.vector.tensor_copy(out=perm[:, P : 2 * P], in_=perm[:, 0:P])
            nc.vector.tensor_copy(out=perm[:, 2 * P : 3 * P], in_=perm[:, 0:P])

            w_grp = stage.tile([P, COUT // P, P, PACK], BF16, align_bytes=64)
            for g in range(COUT // P):
                wtb = psacc.tile([P, PACK, P], BF16, name="acc")
                for t in range(PACK):
                    nc.tensor.transpose(wtb[:, t, :], w_sb[:, g, t:CIN:PACK], ident_bf[:])
                nc.scalar.copy(out=w_grp[:, g], in_=wtb[:].rearrange("p t o -> p o t"))
            btp = pswt.tile([P, P], BF16, name="wt")
            nc.tensor.transpose(btp[:], b_rows[:], ident_bf[:])

            x_parts = []

            def interleave(part, b0, b1, copy):
                if b0 == 0:
                    xg = stage.tile([P, XP, NB, PACK], BF16, align_bytes=64, name="xg", bufs=2)
                    x_parts.append(xg)
                for b in range(b0, b1):
                    copy(out=x_parts[part][:, :, b, :], in_=x_sb[:, part, b].rearrange("p t n -> p n t"))

            def quantise(part):
                n0 = XP * NB * part
                nc.vector.quantize_mx(
                    out=xq[:, n0 : n0 + XP * NB].bitcast(FP8X4),
                    scales=xs[:, n0 : n0 + XP * NB],
                    in_=x_parts[part][:].rearrange("p n b t -> p (n b t)"),
                )

            open_softmax(0)
            exp_first = stage.tile([P, NPART, NB, PCOLS, KK], F32)
            for part in range(NPART):
                cur["exp", part] = exp_first[:, part]

            interleave(0, 0, NB, nc.vector.tensor_copy)
            quantise(0)
            for b in range(NB):
                for half in range(2):
                    column_maximum(0, half, b)
                negate_maximum(b, b + 1, 0, SIDE)
                if b == 0:
                    nc.vector.quantize_mx(
                        out=wq[:].bitcast(FP8X4),
                        scales=wsc[:],
                        in_=w_grp[:].rearrange("p g o t -> p (g o t)"),
                    )
                    nc.vector.tensor_copy(out=bias_sb[:], in_=btp[:, 0 : COUT // P])
                elif b < 3:
                    interleave(1, 2 * b - 2, 2 * b, nc.vector.tensor_copy)
                for part in range(NPART):
                    for m in range(PCOLS):
                        exponential(0, part, b, m)
            quantise(1)
            for part in range(NPART):
                reciprocal_sums(0, part, 0)
                normalise(0, part, 0)
            for v in range(2):
                x3_for_vector(v)
            for v in range(3):
                x3_for_ring(v)
                copy_ring()
            load_logits(1)
            fold_mirrored_columns(0, 0, 0)
            interleave(2, 0, NB, nc.scalar.copy)
            interleave(3, 0, NB, nc.vector.tensor_copy)
            quantise(2)
            quantise(3)
            for step, k in weight_steps[1:]:
                step(0, 0, k)
                copy_weights()

        qvp = ctx.enter_context(tc.tile_pool(name="qvp", bufs=5))
        qsp = ctx.enter_context(tc.tile_pool(name="qsp", bufs=4))
        ssp = ctx.enter_context(tc.tile_pool(name="ssp", bufs=4))
        svp = ctx.enter_context(tc.tile_pool(name="svp", bufs=3))
        outp = ctx.enter_context(tc.tile_pool(name="outp", bufs=2))

        def vector_part(u):
            n, blk, rows, srcs, number, last = bursts[u]
            for i in rows:
                s0, s1 = places_of(u, i)
                if s0 == s1:
                    continue
                qv = qvp.tile([P, GROUP, DX_VEC, CB], F32, name="qv")
                for s in range(s0, s1):
                    dy = srcs[s] - i + PAD
                    nc.vector.tensor_tensor(
                        out=qv[:, s].rearrange("p d (h c) -> p d h c", c=SP),
                        in0=x3_vector[u][:, s, :]
                        .rearrange("p (h c) -> p h c", c=SP)
                        .unsqueeze(1)
                        .to_broadcast([P, DX_VEC, HEADS, SP]),
                        in1=weight_tiles[n][:, KW * dy : KW * dy + DX_VEC, :, i % ROWS]
                        .unsqueeze(3)
                        .to_broadcast([P, DX_VEC, HEADS, SP]),
                        op=ALU.mult,
                    )
                prod_vector[u, i] = qv
            for i in rows:
                s0, s1 = places_of(u, i)
                if s0 == s1:
                    continue
                column = prod_vector[u, i][:, :, DX_VEC - 1, :]
                if number >= SUM_VEC:
                    direct_vector.add((u, i))
                elif (blk, i) in sum_vector:
                    total, first = sum_vector[blk, i]
                    if total is None and s1 - s0 < GROUP:
                        direct_vector.add((u, i))
                    elif total is None:
                        total = svp.tile([P, GROUP, CB], F32, name="sv")
                        sum_vector[blk, i] = (total, None)
                        nc.gpsimd.tensor_tensor(out=total[:], in0=first, in1=column, op=ALU.add)
                    else:
                        nc.gpsimd.tensor_tensor(
                            out=total[:, s0:s1], in0=total[:, s0:s1], in1=column[:, s0:s1], op=ALU.add
                        )
                elif s1 - s0 == GROUP and number + 1 < SUM_VEC:
                    sum_vector[blk, i] = (None, column)
                else:
                    direct_vector.add((u, i))

        def scalar_part(u, between):
            n, blk, rows, srcs, number, last = bursts[u]
            for i in rows:
                if i == rows[1]:
                    between()
                s0, s1 = places_of(u, i)
                if s0 == s1:
                    continue
                starts = (blk, i) not in sum_scalar and s1 - s0 == GROUP
                if starts:
                    qs = ssp.tile([P, GROUP, DX_SCA, CB], F32, name="ss")
                    sum_scalar[blk, i] = qs
                else:
                    qs = qsp.tile([P, GROUP, DX_SCA, CB], F32, name="qs")
                for s in range(s0, s1):
                    dy = srcs[s] - i + PAD
                    for d in range(DX_SCA):
                        for h in range(HEADS):
                            nc.scalar.activation(
                                out=qs[:, s, d, SP * h : SP * h + SP],
                                in_=ring[:, slot(srcs[s]), SP * h : SP * h + SP],
                                func=ACTF.Copy,
                                scale=weight_tiles[n][:, KW * dy + DX_VEC + d, h, i % ROWS : i % ROWS + 1],
                            )
                if starts:
                    pass
                elif (blk, i) in sum_scalar:
                    total = sum_scalar[blk, i]
                    nc.gpsimd.tensor_tensor(out=total[:, s0:s1], in0=total[:, s0:s1], in1=qs[:, s0:s1], op=ALU.add)
                else:
                    direct_scalar.add((u, i))
                    prod_scalar[u, i] = qs
            if last:
                for i in rows:
                    total = sum_scalar[blk, i]
                    nc.gpsimd.tensor_tensor(out=total[:, 0], in0=total[:, 0], in1=total[:, 1], op=ALU.add)

        def add_up(u):
            n, blk, rows, srcs, number, last = bursts[u]

            def transposes(i, terms, closes):
                for t in range(NT):
                    opens = (blk, i, t) not in accs
                    if opens:
                        acc = psacc.tile([P, BANK], F32, name="acc")
                        accs[blk, i, t] = acc
                    for m, (dx, term) in enumerate(terms):
                        shift = NB * (dx - PAD)
                        nc.tensor.matmul(
                            out=accs[blk, i, t][:, 0:P],
                            lhsT=term[:, P * t : P * t + P],
                            rhs=perm[:, P + shift : 2 * P + shift],
                            start=(opens and m == 0),
                            stop=(closes and m == len(terms) - 1),
                            is_transpose=True,
                        )

            if u + 2 < nb:
                x3_for_vector(u + 2)
            if u + 3 < nb:
                x3_for_ring(u + 3)
            for i in rows:
                s0, s1 = places_of(u, i)
                terms = []
                for s in range(s0, s1):
                    if (u, i) in direct_scalar:
                        for d in range(DX_SCA):
                            terms.append((DX_VEC + d, prod_scalar[u, i][:, s, d, :]))
                    for dx in range(DX_VEC - 1):
                        terms.append((dx, prod_vector[u, i][:, s, dx, :]))
                    if (u, i) in direct_vector:
                        terms.append((DX_VEC - 1, prod_vector[u, i][:, s, DX_VEC - 1, :]))
                if last:
                    if (blk, i) in sum_vector:
                        total, first = sum_vector[blk, i]
                        for s in range(GROUP):
                            terms.append((DX_VEC - 1, (first if total is None else total)[:, s, :]))
                    for d in range(DX_SCA):
                        terms.append((DX_VEC + d, sum_scalar[blk, i][:, 0, d, :]))
                transposes(i, terms, last)

        def finish(u, r):
            n, blk, rows, srcs, number, last = bursts[u]
            if not last:
                return
            i = rows[r]
            if r == 0:
                store["rows"] = outp.tile([P, NT, NB, GROUP, SIDE], F32, name="osb")
            for t in range(NT):
                g = NT * blk + t
                nc.scalar.activation(
                    out=store["rows"][:, t, :, r, :],
                    in_=accs[blk, i, t][:, 0:P].rearrange("o (j b) -> o b j", b=NB),
                    func=ACTF.Identity,
                    bias=bias_sb[:, g : g + 1],
                    scale=1.0,
                )
            if r == GROUP - 1:
                for t in range(NT):
                    g = NT * blk + t
                    nc.sync.dma_start(
                        out=out[:, P * g : P * g + P, rows[0] : i + 1, :].rearrange("b o q j -> o b (q j)"),
                        in_=store["rows"][:, t].rearrange("o b q j -> o b (q j)"),
                    )

        vector_part(0)
        for v in range(2):
            scalar_part(v, lambda: None)
        plan = []
        for n, length in enumerate(chunk_bursts):
            plan.extend(make_plan(n, length))
        for u in range(nb):

            def between():
                if u > 0:
                    finish(u - 1, 1)
                copy_weights()

            if u > 0:
                finish(u - 1, 0)
            if u + 1 < nb:
                vector_part(u + 1)
            if u + 2 < nb:
                scalar_part(u + 2, between)
            else:
                between()
            add_up(u)
            copy_ring()
            for step, n, part, k in plan[u]:
                step(n, part, k)
        for r in range(GROUP):
            finish(nb - 1, r)
